import numpy as np
import ml_dtypes


def mxq(x, axis, fmt="e4m3"):
    dtype, down = {"e4m3": (ml_dtypes.float8_e4m3fn, 7), "e5m2": (ml_dtypes.float8_e5m2, 14)}[fmt]
    v = np.moveaxis(np.asarray(x, np.float32).astype(ml_dtypes.bfloat16).astype(np.float64), axis, -1)
    blocks = v.reshape(v.shape[:-1] + (-1, 32))
    amax = np.abs(blocks).max(-1, keepdims=True)
    byte = np.maximum(np.where(amax > 0, np.frexp(amax)[1] - 1 + 127, 0) - down, 1)
    scale = np.exp2(byte - 127.0)
    codes = (blocks / scale).astype(np.float32).astype(dtype).astype(np.float64)
    return np.moveaxis((codes * scale).reshape(v.shape), -1, axis)


WIDE = False


def mx_kscale(k):
    if not WIDE:
        return np.ones(k)
    levels = np.array([20, -20, 10, -10, 0])
    a = np.random.permutation(np.resize(levels, k // 512 * 4)).reshape(k // 512, 4)
    idx = np.arange(k)
    return np.exp2(a[idx // 512, idx % 128 // 32])


BF16 = ml_dtypes.bfloat16


def bf(x):
    return np.asarray(x, np.float32).astype(BF16)


def f64(x):
    return np.asarray(x).astype(np.float64)


B, I, O, NK, ORDER = 8192, 32, 512, 19, 3
K = NK - ORDER


def silu(v):
    return v / (1.0 + np.exp(-v))


def make_knots():
    return np.linspace(-1.0 - 2.0 / NK, 1.0 + 2.0 / NK, NK)


def bases_and_slopes(t, knots, order):
    tb = t[:, None]
    b = ((knots[:-1] <= tb) & (knots[1:] > tb)).astype(np.float64)
    d = np.zeros_like(b)
    for k in range(1, order):
        lw = 1.0 / (knots[k:-1] - knots[:-k - 1])
        rw = 1.0 / (knots[k + 1:] - knots[1:-k])
        lt = (tb - knots[:-k - 1]) * lw
        rt = (knots[k + 1:] - tb) * rw
        d = lw * b[:, :-1] + lt * d[:, :-1] - rw * b[:, 1:] + rt * d[:, 1:]
        b = lt * b[:, :-1] + rt * b[:, 1:]
    return b, d


def setup_inputs():
    u = mx_kscale(O)
    x = np.random.uniform(-1.0, 1.0, (B, I))
    p = np.random.standard_normal((O, I, K)) * 1.5 / np.sqrt(I) / u[:, None, None]
    w_b = (1.0 + 0.1 * np.random.standard_normal(1)) / np.sqrt(I) / u.max()
    w_s = 1.0 + 0.1 * np.random.standard_normal(1)
    g = np.random.standard_normal((B, O)) * np.exp2(np.random.randint(-12, 1, (B, 1))) * 0.25 * u
    return {"x": bf(x),
            "spline_parameters": bf(p),
            "w_b": bf(w_b),
            "w_s": bf(w_s),
            "grad_out": bf(g)}


def reference(x, spline_parameters, w_b, w_s, grad_out):
    x = f64(x)
    g = f64(grad_out)
    p = f64(spline_parameters).reshape(O, I * K)
    m = mxq(g, 1, "e5m2") @ mxq(p, 0, "e4m3")
    slopes = bases_and_slopes(x.reshape(-1), make_knots(), ORDER)[1].reshape(B, I, K)
    spline_part = np.sum(slopes * m.reshape(B, I, K), axis=2)
    sg = 1.0 / (1.0 + np.exp(-x))
    dsilu = sg * (1.0 + x * (1.0 - sg))
    gsum = np.sum(g, axis=1, keepdims=True)
    return f64(w_b) * dsilu * gsum + f64(w_s) * spline_part

@@ -1,0 +1,358 @@
+from contextlib import ExitStack
+
+import concourse.mybir as mybir
+from concourse.masks import make_identity
+
+F32 = mybir.dt.float32
+BF16 = mybir.dt.bfloat16
+U32 = mybir.dt.uint32
+U8 = mybir.dt.uint8
+E4X4 = mybir.dt.float8_e4m3fn_x4
+E5X4 = mybir.dt.float8_e5m2_x4
+ALU = mybir.AluOpType
+ACT = mybir.ActivationFunctionType
+AX = mybir.AxisListType
+
+P = 128
+B, I, O, K = 8192, 32, 512, 16
+NT = B // P
+NJ = K + 1
+W = NJ * I
+GT = 4
+CH = 8
+SC = 16
+NG = NT // GT
+INV_H = 57.0 / 7.0
+G_BUFS = 6
+
+FLOPS = 2 * B * O * I * K
+
+
+def tile_bsplinekanlayer_t_kernel(tc, x, spline_parameters, w_b, w_s, grad_out, out):
+    nc = tc.nc
+    with ExitStack() as ctx:
+        const = ctx.enter_context(tc.tile_pool(name="const", bufs=1))
+        gpool = ctx.enter_context(tc.tile_pool(name="gpool", bufs=G_BUFS))
+        grpool = ctx.enter_context(tc.tile_pool(name="grpool", bufs=3))
+        tpool = ctx.enter_context(tc.tile_pool(name="tpool", bufs=4))
+        ppool = ctx.enter_context(tc.tile_pool(name="ppool", bufs=4))
+        rpool = ctx.enter_context(tc.tile_pool(name="rpool", bufs=4))
+        small = ctx.enter_context(tc.tile_pool(name="small", bufs=2))
+        ps_tp = ctx.enter_context(tc.psum_pool(name="ps_tp", bufs=2))
+        ps_a = ctx.enter_context(tc.psum_pool(name="ps_a", bufs=2))
+        ps_b = ctx.enter_context(tc.psum_pool(name="ps_b", bufs=2))
+        ps_g = ctx.enter_context(tc.psum_pool(name="ps_g", bufs=2))
+        ctx.enter_context(tc.manual_schedule())
+
+        g_view = grad_out.rearrange("(p t) o -> p (t o)", t=NT)
+        out_view = out.rearrange("(p t) i -> p (t i)", t=NT)
+
+        g_nat = {}
+        grp = {}
+        gcode = {}
+        gscale = {}
+        t_tiles = {}
+        p_tiles = {}
+        r_tiles = {}
+        g1_tiles = {}
+        gsb_tiles = {}
+        t1_tiles = {}
+
+        def load_g(gi):
+            g_nat[gi] = gpool.tile([P, GT * O], BF16, name="g_nat")
+            nc.sync.dma_start(out=g_nat[gi][:], in_=g_view[:, gi * GT * O : (gi + 1) * GT * O])
+
+        x_sb = const.tile([P, NT * I], BF16)
+        nc.sync.dma_start(out=x_sb[:], in_=x.rearrange("(p t) i -> p (t i)", t=NT))
+        praw = const.tile([P, 4, O], BF16)
+        p2d = spline_parameters.rearrange("o i k -> o (i k)")
+        for u in range(2):
+            nc.sync.dma_start(
+                out=praw[:, 2 * u : 2 * u + 2, :],
+                in_=p2d[256 * u : 256 * u + 256, :].rearrange("(q e) c -> q e c", e=2),
+            )
+        for gi in range(G_BUFS):
+            load_g(gi)
+        wb_raw = const.tile([P, 1], BF16)
+        ws_raw = const.tile([P, 1], BF16)
+        nc.scalar.dma_start(out=wb_raw[:], in_=w_b.partition_broadcast(P))
+        nc.scalar.dma_start(out=ws_raw[:], in_=w_s.partition_broadcast(P))
+
+        x3 = x_sb[:].rearrange("p (t i) -> p t i", i=I)
+
+        ident = const.tile([P, P], F32)
+        make_identity(nc, ident[:])
+        ones = const.tile([P, 2], BF16)
+        nc.vector.memset(ones[:], 1.0)
+        sel = const.tile([P, 4, P], F32)
+        nc.vector.memset(sel[:], 0.0)
+        a32 = const.tile([P, 32], F32)
+        nc.vector.tensor_reduce(
+            out=a32[:], in_=ident[:].rearrange("p (b t) -> p b t", t=4), axis=AX.X, op=ALU.add
+        )
+        for h in range(4):
+            nc.vector.tensor_copy(out=sel[:, h, 32 * h : 32 * h + 32], in_=a32[:])
+
+        pos = const.tile([P, 4 * O], BF16, align_bytes=64)
+        neg = const.tile([P, 8 * O], BF16, align_bytes=64)
+        nc.gpsimd.memset(neg[:, 0 : 4 * I], 0.0)
+        nc.gpsimd.memset(neg[:, NJ * 4 * I : 8 * O], 0.0)
+        p_perm = praw[:].rearrange("p t (i k) -> p k i t", k=K)
+        nc.vector.tensor_copy(
+            out=pos[:].rearrange("p (j i t) -> p j i t", j=K, i=I, t=4), in_=p_perm
+        )
+        nc.gpsimd.tensor_scalar(
+            out=neg[:, 4 * I : NJ * 4 * I].rearrange("p (j i t) -> p j i t", j=K, i=I, t=4),
+            in0=p_perm,
+            scalar1=-1.0,
+            scalar2=0.0,
+            op0=ALU.mult,
+            op1=ALU.add,
+        )
+        c1 = const.tile([P, O], U32, align_bytes=64)
+        s1 = const.tile([P, O], U8, align_bytes=64)
+        cn = const.tile([P, 2 * O], U32, align_bytes=64)
+        sn = const.tile([P, 2 * O], U8, align_bytes=64)
+        nc.vector.quantize_mx(out=c1[:].bitcast(E4X4), scales=s1[:], in_=pos[:])
+        nc.vector.quantize_mx(out=cn[:].bitcast(E4X4), scales=sn[:], in_=neg[:])
+
+        def abs_instr(c, j):
+            if j == 0:
+                t_tiles[c] = tpool.tile([P, CH, W], F32, name="Tt")
+            nc.scalar.activation(
+                out=t_tiles[c][:, :, I * j : I * j + I],
+                in_=x3[:, c * CH : (c + 1) * CH, :],
+                func=ACT.Abs,
+                scale=INV_H,
+                bias=float(8 - j),
+            )
+
+        tp_tiles = {}
+
+        def transposes(gi):
+            gw = g_nat[gi][:].bitcast(F32)
+            for pair in range(2):
+                tp = ps_tp.tile([P, 2, 2, P], F32, name="tp")
+                tp_tiles[(gi, pair)] = tp
+                for t2 in range(2):
+                    for u in range(2):
+                        col = (2 * pair + t2) * 256 + 128 * u
+                        nc.tensor.transpose(tp[:, t2, u, :], gw[:, col : col + 128], ident[:])
+
+        def copy_out(gi, pair):
+            if pair == 0:
+                grp[gi] = grpool.tile([P, GT * O], BF16, align_bytes=64, name="grp")
+            grp_w = grp[gi][:].bitcast(F32).rearrange("p (t b u) -> p t b u", t=GT, u=2)
+            nc.scalar.copy(
+                out=grp_w[:, 2 * pair : 2 * pair + 2],
+                in_=tp_tiles[(gi, pair)][:].rearrange("p t u b -> p t b u"),
+            )
+
+        def quantise(gi):
+            gcode[gi] = grpool.tile([P, GT * P], U32, align_bytes=64, name="gc")
+            gscale[gi] = grpool.tile([P, GT * P], U8, align_bytes=64, name="gs")
+            nc.vector.quantize_mx(
+                out=gcode[gi][:].bitcast(E5X4), scales=gscale[gi][:], in_=grp[gi][:]
+            )
+
+        def row_sums(gi):
+            k = gi // 4
+            if gi % 4 == 0:
+                g1_tiles[k] = ps_g.tile([P, 5 * SC], F32, name="g1")
+            for t4 in range(GT):
+                tl = (gi % 4) * GT + t4
+                for h in range(4):
+                    col = h * SC + tl
+                    nc.tensor.matmul(
+                        out=g1_tiles[k][:, col : col + 1],
+                        lhsT=grp[gi][:, O * t4 + P * h : O * t4 + P * h + P],
+                        rhs=ones[:, 0:1],
+                        start=True,
+                        stop=True,
+                    )
+
+        def mx_tile(gi, t4):
+            cols = slice(P * t4, P * t4 + P)
+            lhs = gcode[gi][:, cols].bitcast(E5X4)
+            lhs_s = gscale[gi][:, cols]
+            bank_a = ps_a.tile([P, O], F32, name="bank_a")
+            nc.tensor.matmul_mx(
+                out=bank_a[:], lhsT=lhs, lhsT_scale=lhs_s,
+                rhs=c1[:].bitcast(E4X4), rhs_scale=s1[:], start=True, stop=False,
+            )
+            nc.tensor.matmul_mx(
+                out=bank_a[:], lhsT=lhs, lhsT_scale=lhs_s,
+                rhs=cn[:, 0:O].bitcast(E4X4), rhs_scale=sn[:, 0:O], start=False, stop=True,
+            )
+            bank_b = ps_b.tile([P, O], F32, name="bank_b")
+            nc.tensor.matmul_mx(
+                out=bank_b[:], lhsT=lhs, lhsT_scale=lhs_s,
+                rhs=cn[:, O : 2 * O].bitcast(E4X4), rhs_scale=sn[:, O : 2 * O], start=True, stop=True,
+            )
+            if t4 == 0:
+                p_tiles[gi] = ppool.tile([P, GT, W], F32, name="p_t")
+            tile_no = gi * GT + t4
+            t_tile = t_tiles[tile_no // CH]
+            tl = tile_no % CH
+            nc.vector.scalar_tensor_tensor(
+                out=p_tiles[gi][:, t4, 0:O], in0=t_tile[:, tl, 0:O], scalar=1.0, in1=bank_a[:],
+                op0=ALU.min, op1=ALU.mult,
+            )
+            nc.vector.scalar_tensor_tensor(
+                out=p_tiles[gi][:, t4, O:W], in0=t_tile[:, tl, O:W], scalar=1.0, in1=bank_b[:, 0:I],
+                op0=ALU.min, op1=ALU.mult,
+            )
+
+        def r_slice(gi, first):
+            k = gi // 4
+            if k not in r_tiles:
+                r_tiles[k] = rpool.tile([P, SC * I], F32, name="r_k")
+            col = ((gi % 4) * GT + first) * I
+            return r_tiles[k][:, col : col + 2 * I].rearrange("p (t i) -> p t i", i=I)
+
+        def tree_reduce(gi):
+            p_t = p_tiles[gi]
+            for half in (256, 128, 64, 32):
+                nc.gpsimd.tensor_tensor(
+                    out=p_t[:, 0:2, 0:half], in0=p_t[:, 0:2, 0:half], in1=p_t[:, 0:2, half : 2 * half],
+                    op=ALU.add,
+                )
+            nc.gpsimd.tensor_tensor(
+                out=r_slice(gi, 0), in0=p_t[:, 0:2, 0:I], in1=p_t[:, 0:2, O:W], op=ALU.add
+            )
+
+        def vector_reduce(gi):
+            nc.vector.tensor_reduce(
+                out=r_slice(gi, 2),
+                in_=p_tiles[gi][:, 2:4, :].rearrange("p t (j i) -> p t i j", i=I),
+                axis=AX.X,
+                op=ALU.add,
+            )
+
+        th = const.tile([P, NT * I], F32)
+        q = const.tile([P, NT * I], F32)
+        dsw = const.tile([P, NT * I], F32)
+        hwb = const.tile([P, 1], F32)
+        nqwb = const.tile([P, 1], F32)
+        pqwb = const.tile([P, 1], F32)
+        wsn = const.tile([P, 1], F32)
+        HALF = NT * I // 2
+
+        def dsilu_op(n):
+            cs = slice((n // 5) * HALF, (n // 5 + 1) * HALF)
+            step = n % 5
+            if step == 0:
+                nc.gpsimd.tensor_tensor(out=q[:, cs], in0=th[:, cs], in1=th[:, cs], op=ALU.mult)
+            elif step == 1:
+                nc.gpsimd.tensor_scalar(
+                    out=q[:, cs], in0=q[:, cs], scalar1=nqwb[:, 0:1], scalar2=pqwb[:, 0:1],
+                    op0=ALU.mult, op1=ALU.add,
+                )
+            elif step == 2:
+                nc.gpsimd.tensor_tensor(out=q[:, cs], in0=q[:, cs], in1=x_sb[:, cs], op=ALU.mult)
+            elif step == 3:
+                nc.gpsimd.tensor_scalar(
+                    out=th[:, cs], in0=th[:, cs], scalar1=hwb[:, 0:1], scalar2=hwb[:, 0:1],
+                    op0=ALU.mult, op1=ALU.add,
+                )
+            else:
+                nc.gpsimd.tensor_tensor(out=dsw[:, cs], in0=q[:, cs], in1=th[:, cs], op=ALU.add)
+
+        def sums_to_rows_a(k):
+            g1s = small.tile([P, 4 * SC], F32, name="g1s")
+            nc.scalar.copy(out=g1s[:], in_=g1_tiles[k][:, 0 : 4 * SC])
+            return g1s
+
+        def sums_to_rows_b(k, g1s):
+            for h in range(4):
+                nc.tensor.matmul(
+                    out=g1_tiles[k][:, 4 * SC : 5 * SC], lhsT=sel[:, h, :],
+                    rhs=g1s[:, h * SC : (h + 1) * SC], start=(h == 0), stop=(h == 3),
+                )
+            gsb_tiles[k] = rpool.tile([P, SC], F32, name="gsb")
+            nc.scalar.copy(out=gsb_tiles[k][:], in_=g1_tiles[k][:, 4 * SC : 5 * SC])
+
+        def silu_term(k):
+            t1_tiles[k] = small.tile([P, SC, I], F32, name="t1")
+            nc.vector.tensor_tensor(
+                out=t1_tiles[k][:],
+                in0=dsw[:, k * SC * I : (k + 1) * SC * I].rearrange("p (t i) -> p t i", i=I),
+                in1=gsb_tiles[k][:].unsqueeze(2).to_broadcast([P, SC, I]),
+                op=ALU.mult,
+            )
+
+        def finish(k, half):
+            n = SC * I // 2
+            o_c = small.tile([P, n], F32, name="o_c")
+            nc.vector.scalar_tensor_tensor(
+                out=o_c[:],
+                in0=r_tiles[k][:, half * n : (half + 1) * n],
+                scalar=wsn[:, 0:1],
+                in1=t1_tiles[k][:].rearrange("p t i -> p (t i)")[:, half * n : (half + 1) * n],
+                op0=ALU.mult,
+                op1=ALU.add,
+            )
+            c0 = k * SC * I + half * n
+            nc.sync.dma_start(out=out_view[:, c0 : c0 + n], in_=o_c[:])
+
+        transposes(0)
+        for j in range(10):
+            abs_instr(0, j)
+        copy_out(0, 0)
+        copy_out(0, 1)
+        for j in range(10, NJ):
+            abs_instr(0, j)
+        quantise(0)
+        nc.vector.tensor_scalar(out=hwb[:], in0=wb_raw[:], scalar1=0.5, scalar2=None, op0=ALU.mult)
+        nc.vector.tensor_scalar(out=nqwb[:], in0=wb_raw[:], scalar1=-0.25, scalar2=None, op0=ALU.mult)
+        nc.vector.tensor_scalar(out=pqwb[:], in0=wb_raw[:], scalar1=0.25, scalar2=None, op0=ALU.mult)
+        nc.vector.tensor_scalar(out=wsn[:], in0=ws_raw[:], scalar1=-INV_H, scalar2=None, op0=ALU.mult)
+
+        finish_at = {7: 0, 9: 1, 12: 2}
+
+        for gi in range(NG):
+            if gi + G_BUFS < NG:
+                load_g(gi + G_BUFS)
+            c_next = gi // 2 + 1
+            fill = []
+            if c_next < NT // CH:
+                fill = list(range(0, 9)) if gi % 2 == 0 else list(range(9, NJ))
+            nxt = gi + 1
+            if nxt < NG:
+                transposes(nxt)
+            for j in fill[0:3]:
+                abs_instr(c_next, j)
+            if nxt < NG:
+                copy_out(nxt, 0)
+            for j in fill[3:5]:
+                abs_instr(c_next, j)
+            if nxt < NG:
+                copy_out(nxt, 1)
+            row_sums(gi)
+            g1s = None
+            if gi % 4 == 3:
+                g1s = sums_to_rows_a(gi // 4)
+            for j in fill[5:]:
+                abs_instr(c_next, j)
+            if gi == 0:
+                nc.scalar.activation(out=th[:], in_=x_sb[:], func=ACT.Tanh, scale=0.5)
+            for t4 in range(GT):
+                mx_tile(gi, t4)
+                if t4 == 1:
+                    if nxt < NG:
+                        quantise(nxt)
+                    tree_reduce(gi)
+                    if gi % 4 == 3:
+                        sums_to_rows_b(gi // 4, g1s)
+                if t4 == 2 and gi == NG - 1:
+                    silu_term(3)
+                    finish(3, 0)
+            vector_reduce(gi)
+            if 1 <= gi <= 10:
+                dsilu_op(gi - 1)
+            if gi in finish_at:
+                k = finish_at[gi]
+                silu_term(k)
+                finish(k, 0)
+                finish(k, 1)
+        finish(3, 1)

@@ -203,28 +203,17 @@ def tile_bsplinekanlayer_t_kernel(tc, x, spline_parameters, w_b, w_s, grad_out, 
                 op0=ALU.min, op1=ALU.mult,
             )
 
-        def r_slice(gi, first):
+        def r_slice(gi, first, count):
             k = gi // 4
             if k not in r_tiles:
                 r_tiles[k] = rpool.tile([P, SC * I], F32, name="r_k")
             col = ((gi % 4) * GT + first) * I
-            return r_tiles[k][:, col : col + 2 * I].rearrange("p (t i) -> p t i", i=I)
-
-        def tree_reduce(gi):
-            p_t = p_tiles[gi]
-            for half in (256, 128, 64, 32):
-                nc.gpsimd.tensor_tensor(
-                    out=p_t[:, 0:2, 0:half], in0=p_t[:, 0:2, 0:half], in1=p_t[:, 0:2, half : 2 * half],
-                    op=ALU.add,
-                )
-            nc.gpsimd.tensor_tensor(
-                out=r_slice(gi, 0), in0=p_t[:, 0:2, 0:I], in1=p_t[:, 0:2, O:W], op=ALU.add
-            )
+            return r_tiles[k][:, col : col + count * I].rearrange("p (t i) -> p t i", i=I)
 
         def vector_reduce(gi):
             nc.vector.tensor_reduce(
-                out=r_slice(gi, 2),
-                in_=p_tiles[gi][:, 2:4, :].rearrange("p t (j i) -> p t i j", i=I),
+                out=r_slice(gi, 0, GT),
+                in_=p_tiles[gi][:].rearrange("p t (j i) -> p t i j", i=I),
                 axis=AX.X,
                 op=ALU.add,
             )
@@ -238,25 +227,26 @@ def tile_bsplinekanlayer_t_kernel(tc, x, spline_parameters, w_b, w_s, grad_out, 
         wsn = const.tile([P, 1], F32)
         HALF = NT * I // 2
 
-        def dsilu_op(n):
-            cs = slice((n // 5) * HALF, (n // 5 + 1) * HALF)
-            step = n % 5
+        def dsilu_scalar(step):
             if step == 0:
-                nc.gpsimd.tensor_tensor(out=q[:, cs], in0=th[:, cs], in1=th[:, cs], op=ALU.mult)
+                nc.scalar.activation(out=th[:], in_=x_sb[:], func=ACT.Tanh, scale=0.5)
             elif step == 1:
-                nc.gpsimd.tensor_scalar(
-                    out=q[:, cs], in0=q[:, cs], scalar1=nqwb[:, 0:1], scalar2=pqwb[:, 0:1],
-                    op0=ALU.mult, op1=ALU.add,
-                )
+                nc.scalar.activation(out=q[:], in_=th[:], func=ACT.Square)
             elif step == 2:
-                nc.gpsimd.tensor_tensor(out=q[:, cs], in0=q[:, cs], in1=x_sb[:, cs], op=ALU.mult)
-            elif step == 3:
-                nc.gpsimd.tensor_scalar(
-                    out=th[:, cs], in0=th[:, cs], scalar1=hwb[:, 0:1], scalar2=hwb[:, 0:1],
-                    op0=ALU.mult, op1=ALU.add,
+                nc.scalar.activation(
+                    out=q[:], in_=q[:], func=ACT.Identity, scale=nqwb[:, 0:1], bias=pqwb[:, 0:1]
                 )
             else:
-                nc.gpsimd.tensor_tensor(out=dsw[:, cs], in0=q[:, cs], in1=th[:, cs], op=ALU.add)
+                nc.scalar.activation(
+                    out=th[:], in_=th[:], func=ACT.Identity, scale=hwb[:, 0:1], bias=hwb[:, 0:1]
+                )
+
+        def dsilu_vector(n):
+            cs = slice((n // 2) * HALF, (n // 2 + 1) * HALF)
+            if n % 2 == 0:
+                nc.vector.tensor_tensor(out=q[:, cs], in0=q[:, cs], in1=x_sb[:, cs], op=ALU.mult)
+            else:
+                nc.vector.tensor_tensor(out=dsw[:, cs], in0=q[:, cs], in1=th[:, cs], op=ALU.add)
 
         def sums_to_rows_a(k):
             g1s = small.tile([P, 4 * SC], F32, name="g1s")
@@ -334,22 +324,21 @@ def tile_bsplinekanlayer_t_kernel(tc, x, spline_parameters, w_b, w_s, grad_out, 
                 g1s = sums_to_rows_a(gi // 4)
             for j in fill[5:]:
                 abs_instr(c_next, j)
-            if gi == 0:
-                nc.scalar.activation(out=th[:], in_=x_sb[:], func=ACT.Tanh, scale=0.5)
+            if 1 <= gi <= 4:
+                dsilu_scalar(gi - 1)
             for t4 in range(GT):
                 mx_tile(gi, t4)
                 if t4 == 1:
                     if nxt < NG:
                         quantise(nxt)
-                    tree_reduce(gi)
                     if gi % 4 == 3:
                         sums_to_rows_b(gi // 4, g1s)
                 if t4 == 2 and gi == NG - 1:
                     silu_term(3)
                     finish(3, 0)
             vector_reduce(gi)
-            if 1 <= gi <= 10:
-                dsilu_op(gi - 1)
+            if 5 <= gi <= 8:
+                dsilu_vector(gi - 5)
             if gi in finish_at:
                 k = finish_at[gi]
                 silu_term(k)

@@ -24,6 +24,8 @@ SC = 16
 NG = NT // GT
 INV_H = 57.0 / 7.0
 G_BUFS = 6
+BSTEP = 64
+LAST0 = (GT - 1) * BSTEP
 
 FLOPS = 2 * B * O * I * K
 
@@ -39,8 +41,8 @@ def tile_bsplinekanlayer_t_kernel(tc, x, spline_parameters, w_b, w_s, grad_out, 
         rpool = ctx.enter_context(tc.tile_pool(name="rpool", bufs=4))
         small = ctx.enter_context(tc.tile_pool(name="small", bufs=2))
         ps_tp = ctx.enter_context(tc.psum_pool(name="ps_tp", bufs=2))
-        ps_a = ctx.enter_context(tc.psum_pool(name="ps_a", bufs=2))
-        ps_b = ctx.enter_context(tc.psum_pool(name="ps_b", bufs=2))
+        ps_a = ctx.enter_context(tc.psum_pool(name="ps_a", bufs=3))
+        ps_b = ctx.enter_context(tc.psum_pool(name="ps_b", bufs=1))
         ps_g = ctx.enter_context(tc.psum_pool(name="ps_g", bufs=2))
         ctx.enter_context(tc.manual_schedule())
 
@@ -94,16 +96,25 @@ def tile_bsplinekanlayer_t_kernel(tc, x, spline_parameters, w_b, w_s, grad_out, 
             nc.vector.tensor_copy(out=sel[:, h, 32 * h : 32 * h + 32], in_=a32[:])
 
         pos = const.tile([P, 4 * O], BF16, align_bytes=64)
-        neg = const.tile([P, 8 * O], BF16, align_bytes=64)
+        neg = const.tile([P, 4 * O], BF16, align_bytes=64)
+        last = const.tile([P, 8 * O], BF16, align_bytes=64)
         nc.gpsimd.memset(neg[:, 0 : 4 * I], 0.0)
-        nc.gpsimd.memset(neg[:, NJ * 4 * I : 8 * O], 0.0)
+        nc.gpsimd.memset(last[:], 0.0)
         p_perm = praw[:].rearrange("p t (i k) -> p k i t", k=K)
         nc.vector.tensor_copy(
             out=pos[:].rearrange("p (j i t) -> p j i t", j=K, i=I, t=4), in_=p_perm
         )
         nc.gpsimd.tensor_scalar(
-            out=neg[:, 4 * I : NJ * 4 * I].rearrange("p (j i t) -> p j i t", j=K, i=I, t=4),
-            in0=p_perm,
+            out=neg[:, 4 * I : 4 * O].rearrange("p (j i t) -> p j i t", j=K - 1, i=I, t=4),
+            in0=p_perm[:, 0 : K - 1],
+            scalar1=-1.0,
+            scalar2=0.0,
+            op0=ALU.mult,
+            op1=ALU.add,
+        )
+        nc.gpsimd.tensor_scalar(
+            out=last[:, 4 * LAST0 : 4 * LAST0 + 4 * I].rearrange("p (i t) -> p i t", t=4),
+            in0=p_perm[:, K - 1],
             scalar1=-1.0,
             scalar2=0.0,
             op0=ALU.mult,
@@ -111,10 +122,13 @@ def tile_bsplinekanlayer_t_kernel(tc, x, spline_parameters, w_b, w_s, grad_out, 
         )
         c1 = const.tile([P, O], U32, align_bytes=64)
         s1 = const.tile([P, O], U8, align_bytes=64)
-        cn = const.tile([P, 2 * O], U32, align_bytes=64)
-        sn = const.tile([P, 2 * O], U8, align_bytes=64)
+        cn = const.tile([P, O], U32, align_bytes=64)
+        sn = const.tile([P, O], U8, align_bytes=64)
+        cl = const.tile([P, 2 * O], U32, align_bytes=64)
+        sl = const.tile([P, 2 * O], U8, align_bytes=64)
         nc.vector.quantize_mx(out=c1[:].bitcast(E4X4), scales=s1[:], in_=pos[:])
         nc.vector.quantize_mx(out=cn[:].bitcast(E4X4), scales=sn[:], in_=neg[:])
+        nc.vector.quantize_mx(out=cl[:].bitcast(E4X4), scales=sl[:], in_=last[:])
 
         def abs_instr(c, j):
             if j == 0:
@@ -171,6 +185,8 @@ def tile_bsplinekanlayer_t_kernel(tc, x, spline_parameters, w_b, w_s, grad_out, 
                         stop=True,
                     )
 
+        bank_b = {}
+
         def mx_tile(gi, t4):
             cols = slice(P * t4, P * t4 + P)
             lhs = gcode[gi][:, cols].bitcast(E5X4)
@@ -182,12 +198,15 @@ def tile_bsplinekanlayer_t_kernel(tc, x, spline_parameters, w_b, w_s, grad_out, 
             )
             nc.tensor.matmul_mx(
                 out=bank_a[:], lhsT=lhs, lhsT_scale=lhs_s,
-                rhs=cn[:, 0:O].bitcast(E4X4), rhs_scale=sn[:, 0:O], start=False, stop=True,
+                rhs=cn[:].bitcast(E4X4), rhs_scale=sn[:], start=False, stop=True,
             )
-            bank_b = ps_b.tile([P, O], F32, name="bank_b")
+            if t4 == 0:
+                bank_b[gi] = ps_b.tile([P, O], F32, name="bank_b")
+            w0 = LAST0 - BSTEP * t4
             nc.tensor.matmul_mx(
-                out=bank_b[:], lhsT=lhs, lhsT_scale=lhs_s,
-                rhs=cn[:, O : 2 * O].bitcast(E4X4), rhs_scale=sn[:, O : 2 * O], start=True, stop=True,
+                out=bank_b[gi][:], lhsT=lhs, lhsT_scale=lhs_s,
+                rhs=cl[:, w0 : w0 + O].bitcast(E4X4), rhs_scale=sl[:, w0 : w0 + O],
+                start=(t4 == 0), stop=(t4 == GT - 1),
             )
             if t4 == 0:
                 p_tiles[gi] = ppool.tile([P, GT, W], F32, name="p_t")
@@ -198,10 +217,14 @@ def tile_bsplinekanlayer_t_kernel(tc, x, spline_parameters, w_b, w_s, grad_out, 
                 out=p_tiles[gi][:, t4, 0:O], in0=t_tile[:, tl, 0:O], scalar=1.0, in1=bank_a[:],
                 op0=ALU.min, op1=ALU.mult,
             )
-            nc.vector.scalar_tensor_tensor(
-                out=p_tiles[gi][:, t4, O:W], in0=t_tile[:, tl, O:W], scalar=1.0, in1=bank_b[:, 0:I],
-                op0=ALU.min, op1=ALU.mult,
-            )
+            if t4 == GT - 1:
+                nc.vector.scalar_tensor_tensor(
+                    out=p_tiles[gi][:, :, O:W],
+                    in0=t_tile[:, tl - (GT - 1) : tl + 1, O:W],
+                    scalar=1.0,
+                    in1=bank_b[gi][:, 0 : GT * BSTEP].rearrange("p (t c) -> p t c", c=BSTEP)[:, :, 0:I],
+                    op0=ALU.min, op1=ALU.mult,
+                )
 
         def r_slice(gi, first, count):
             k = gi // 4
@@ -210,12 +233,17 @@ def tile_bsplinekanlayer_t_kernel(tc, x, spline_parameters, w_b, w_s, grad_out, 
             col = ((gi % 4) * GT + first) * I
             return r_tiles[k][:, col : col + count * I].rearrange("p (t i) -> p t i", i=I)
 
-        def vector_reduce(gi):
-            nc.vector.tensor_reduce(
-                out=r_slice(gi, 0, GT),
-                in_=p_tiles[gi][:].rearrange("p t (j i) -> p t i j", i=I),
-                axis=AX.X,
+        def halve(eng, gi, t0, t1, half):
+            p_t = p_tiles[gi]
+            eng.tensor_tensor(
+                out=p_t[:, t0:t1, 0:half], in0=p_t[:, t0:t1, 0:half], in1=p_t[:, t0:t1, half : 2 * half],
                 op=ALU.add,
+            )
+
+        def last_add(eng, gi, t0, t1):
+            p_t = p_tiles[gi]
+            eng.tensor_tensor(
+                out=r_slice(gi, t0, t1 - t0), in0=p_t[:, t0:t1, 0:I], in1=p_t[:, t0:t1, O:W], op=ALU.add
             )
 
         th = const.tile([P, NT * I], F32)
@@ -331,12 +359,25 @@ def tile_bsplinekanlayer_t_kernel(tc, x, spline_parameters, w_b, w_s, grad_out, 
                 if t4 == 1:
                     if nxt < NG:
                         quantise(nxt)
+                    halve(nc.gpsimd, gi, 0, 2, 256)
+                    if gi == NG - 1:
+                        for half in (128, 64, 32):
+                            halve(nc.gpsimd, gi, 0, 2, half)
                     if gi % 4 == 3:
                         sums_to_rows_b(gi // 4, g1s)
                 if t4 == 2 and gi == NG - 1:
                     silu_term(3)
                     finish(3, 0)
-            vector_reduce(gi)
+            halve(nc.vector, gi, 2, 4, 256)
+            if gi < NG - 1:
+                for half in (128, 64, 32):
+                    halve(nc.gpsimd, gi, 0, 4, half)
+                last_add(nc.gpsimd, gi, 0, 4)
+            else:
+                last_add(nc.gpsimd, gi, 0, 2)
+                for half in (128, 64, 32):
+                    halve(nc.vector, gi, 2, 4, half)
+                last_add(nc.vector, gi, 2, 4)
             if 5 <= gi <= 8:
                 dsilu_vector(gi - 5)
             if gi in finish_at:

@@ -359,25 +359,16 @@ def tile_bsplinekanlayer_t_kernel(tc, x, spline_parameters, w_b, w_s, grad_out, 
                 if t4 == 1:
                     if nxt < NG:
                         quantise(nxt)
-                    halve(nc.gpsimd, gi, 0, 2, 256)
-                    if gi == NG - 1:
-                        for half in (128, 64, 32):
-                            halve(nc.gpsimd, gi, 0, 2, half)
                     if gi % 4 == 3:
                         sums_to_rows_b(gi // 4, g1s)
                 if t4 == 2 and gi == NG - 1:
                     silu_term(3)
                     finish(3, 0)
-            halve(nc.vector, gi, 2, 4, 256)
-            if gi < NG - 1:
-                for half in (128, 64, 32):
-                    halve(nc.gpsimd, gi, 0, 4, half)
-                last_add(nc.gpsimd, gi, 0, 4)
-            else:
-                last_add(nc.gpsimd, gi, 0, 2)
-                for half in (128, 64, 32):
-                    halve(nc.vector, gi, 2, 4, half)
-                last_add(nc.vector, gi, 2, 4)
+            halve(nc.vector, gi, 0, 4, 256)
+            rest = nc.gpsimd if gi < NG - 1 else nc.vector
+            for half in (128, 64, 32):
+                halve(rest, gi, 0, 4, half)
+            last_add(rest, gi, 0, 4)
             if 5 <= gi <= 8:
                 dsilu_vector(gi - 5)
             if gi in finish_at:

@@ -365,10 +365,9 @@ def tile_bsplinekanlayer_t_kernel(tc, x, spline_parameters, w_b, w_s, grad_out, 
                     silu_term(3)
                     finish(3, 0)
             halve(nc.vector, gi, 0, 4, 256)
-            rest = nc.gpsimd if gi < NG - 1 else nc.vector
             for half in (128, 64, 32):
-                halve(rest, gi, 0, 4, half)
-            last_add(rest, gi, 0, 4)
+                halve(nc.vector, gi, 0, 4, half)
+            last_add(nc.vector, gi, 0, 4)
             if 5 <= gi <= 8:
                 dsilu_vector(gi - 5)
             if gi in finish_at:

@@ -7,6 +7,7 @@ F32 = mybir.dt.float32
 BF16 = mybir.dt.bfloat16
 U32 = mybir.dt.uint32
 U8 = mybir.dt.uint8
+I32 = mybir.dt.int32
 E4X4 = mybir.dt.float8_e4m3fn_x4
 E5X4 = mybir.dt.float8_e5m2_x4
 ALU = mybir.AluOpType
@@ -41,9 +42,9 @@ def tile_bsplinekanlayer_t_kernel(tc, x, spline_parameters, w_b, w_s, grad_out, 
         rpool = ctx.enter_context(tc.tile_pool(name="rpool", bufs=4))
         small = ctx.enter_context(tc.tile_pool(name="small", bufs=2))
         ps_tp = ctx.enter_context(tc.psum_pool(name="ps_tp", bufs=2))
-        ps_a = ctx.enter_context(tc.psum_pool(name="ps_a", bufs=3))
+        ps_a = ctx.enter_context(tc.psum_pool(name="ps_a", bufs=4))
         ps_b = ctx.enter_context(tc.psum_pool(name="ps_b", bufs=1))
-        ps_g = ctx.enter_context(tc.psum_pool(name="ps_g", bufs=2))
+        ps_g = ctx.enter_context(tc.psum_pool(name="ps_g", bufs=1))
         ctx.enter_context(tc.manual_schedule())
 
         g_view = grad_out.rearrange("(p t) o -> p (t o)", t=NT)
@@ -65,7 +66,8 @@ def tile_bsplinekanlayer_t_kernel(tc, x, spline_parameters, w_b, w_s, grad_out, 
             nc.sync.dma_start(out=g_nat[gi][:], in_=g_view[:, gi * GT * O : (gi + 1) * GT * O])
 
         x_sb = const.tile([P, NT * I], BF16)
-        nc.sync.dma_start(out=x_sb[:], in_=x.rearrange("(p t) i -> p (t i)", t=NT))
+        x_view = x.rearrange("(p t) i -> p (t i)", t=NT)
+        nc.sync.dma_start(out=x_sb[:, 0 : CH * I], in_=x_view[:, 0 : CH * I])
         praw = const.tile([P, 4, O], BF16)
         p2d = spline_parameters.rearrange("o i k -> o (i k)")
         for u in range(2):
@@ -73,7 +75,9 @@ def tile_bsplinekanlayer_t_kernel(tc, x, spline_parameters, w_b, w_s, grad_out, 
                 out=praw[:, 2 * u : 2 * u + 2, :],
                 in_=p2d[256 * u : 256 * u + 256, :].rearrange("(q e) c -> q e c", e=2),
             )
-        for gi in range(G_BUFS):
+        load_g(0)
+        nc.sync.dma_start(out=x_sb[:, CH * I : NT * I], in_=x_view[:, CH * I : NT * I])
+        for gi in range(1, G_BUFS):
             load_g(gi)
         wb_raw = const.tile([P, 1], BF16)
         ws_raw = const.tile([P, 1], BF16)
@@ -97,9 +101,12 @@ def tile_bsplinekanlayer_t_kernel(tc, x, spline_parameters, w_b, w_s, grad_out, 
 
         pos = const.tile([P, 4 * O], BF16, align_bytes=64)
         neg = const.tile([P, 4 * O], BF16, align_bytes=64)
-        last = const.tile([P, 8 * O], BF16, align_bytes=64)
+        last = const.tile([P, 4 * I], BF16, align_bytes=64)
+        cl = const.tile([P, 2 * O], U32, align_bytes=64)
+        sl = const.tile([P, 2 * O], U8, align_bytes=64)
+        nc.vector.memset(cl[:].bitcast(I32), 0)
+        nc.vector.memset(sl[:].bitcast(I32), 0)
         nc.gpsimd.memset(neg[:, 0 : 4 * I], 0.0)
-        nc.gpsimd.memset(last[:], 0.0)
         p_perm = praw[:].rearrange("p t (i k) -> p k i t", k=K)
         nc.vector.tensor_copy(
             out=pos[:].rearrange("p (j i t) -> p j i t", j=K, i=I, t=4), in_=p_perm
@@ -112,30 +119,29 @@ def tile_bsplinekanlayer_t_kernel(tc, x, spline_parameters, w_b, w_s, grad_out, 
             op0=ALU.mult,
             op1=ALU.add,
         )
-        nc.gpsimd.tensor_scalar(
-            out=last[:, 4 * LAST0 : 4 * LAST0 + 4 * I].rearrange("p (i t) -> p i t", t=4),
+        nc.vector.tensor_scalar(
+            out=last[:].rearrange("p (i t) -> p i t", t=4),
             in0=p_perm[:, K - 1],
             scalar1=-1.0,
-            scalar2=0.0,
+            scalar2=None,
             op0=ALU.mult,
-            op1=ALU.add,
         )
         c1 = const.tile([P, O], U32, align_bytes=64)
         s1 = const.tile([P, O], U8, align_bytes=64)
         cn = const.tile([P, O], U32, align_bytes=64)
         sn = const.tile([P, O], U8, align_bytes=64)
-        cl = const.tile([P, 2 * O], U32, align_bytes=64)
-        sl = const.tile([P, 2 * O], U8, align_bytes=64)
         nc.vector.quantize_mx(out=c1[:].bitcast(E4X4), scales=s1[:], in_=pos[:])
         nc.vector.quantize_mx(out=cn[:].bitcast(E4X4), scales=sn[:], in_=neg[:])
-        nc.vector.quantize_mx(out=cl[:].bitcast(E4X4), scales=sl[:], in_=last[:])
+        nc.vector.quantize_mx(
+            out=cl[:, LAST0 : LAST0 + I].bitcast(E4X4), scales=sl[:, LAST0 : LAST0 + I], in_=last[:]
+        )
 
-        def abs_instr(c, j):
-            if j == 0:
+        def abs_instr(c, j, lo=0, hi=CH):
+            if c not in t_tiles:
                 t_tiles[c] = tpool.tile([P, CH, W], F32, name="Tt")
             nc.scalar.activation(
-                out=t_tiles[c][:, :, I * j : I * j + I],
-                in_=x3[:, c * CH : (c + 1) * CH, :],
+                out=t_tiles[c][:, lo:hi, I * j : I * j + I],
+                in_=x3[:, c * CH + lo : c * CH + hi, :],
                 func=ACT.Abs,
                 scale=INV_H,
                 bias=float(8 - j),
@@ -255,26 +261,28 @@ def tile_bsplinekanlayer_t_kernel(tc, x, spline_parameters, w_b, w_s, grad_out, 
         wsn = const.tile([P, 1], F32)
         HALF = NT * I // 2
 
-        def dsilu_scalar(step):
+        def dsilu_scalar(k, step):
+            cs = slice(k * SC * I, (k + 1) * SC * I)
             if step == 0:
-                nc.scalar.activation(out=th[:], in_=x_sb[:], func=ACT.Tanh, scale=0.5)
+                nc.scalar.activation(out=th[:, cs], in_=x_sb[:, cs], func=ACT.Tanh, scale=0.5)
             elif step == 1:
-                nc.scalar.activation(out=q[:], in_=th[:], func=ACT.Square)
+                nc.scalar.activation(out=q[:, cs], in_=th[:, cs], func=ACT.Square)
             elif step == 2:
                 nc.scalar.activation(
-                    out=q[:], in_=q[:], func=ACT.Identity, scale=nqwb[:, 0:1], bias=pqwb[:, 0:1]
+                    out=q[:, cs], in_=q[:, cs], func=ACT.Identity, scale=nqwb[:, 0:1], bias=pqwb[:, 0:1]
                 )
             else:
                 nc.scalar.activation(
-                    out=th[:], in_=th[:], func=ACT.Identity, scale=hwb[:, 0:1], bias=hwb[:, 0:1]
+                    out=th[:, cs], in_=th[:, cs], func=ACT.Identity, scale=hwb[:, 0:1], bias=hwb[:, 0:1]
                 )
 
-        def dsilu_vector(n):
-            cs = slice((n // 2) * HALF, (n // 2 + 1) * HALF)
-            if n % 2 == 0:
-                nc.vector.tensor_tensor(out=q[:, cs], in0=q[:, cs], in1=x_sb[:, cs], op=ALU.mult)
-            else:
-                nc.vector.tensor_tensor(out=dsw[:, cs], in0=q[:, cs], in1=th[:, cs], op=ALU.add)
+        def dsilu_mult(k):
+            cs = slice(k * SC * I, (k + 1) * SC * I)
+            nc.gpsimd.tensor_tensor(out=q[:, cs], in0=q[:, cs], in1=x_sb[:, cs], op=ALU.mult)
+
+        def dsilu_add(k):
+            cs = slice(k * SC * I, (k + 1) * SC * I)
+            nc.vector.tensor_tensor(out=dsw[:, cs], in0=q[:, cs], in1=th[:, cs], op=ALU.add)
 
         def sums_to_rows_a(k):
             g1s = small.tile([P, 4 * SC], F32, name="g1s")
@@ -292,12 +300,12 @@ def tile_bsplinekanlayer_t_kernel(tc, x, spline_parameters, w_b, w_s, grad_out, 
 
         def silu_term(k):
             t1_tiles[k] = small.tile([P, SC, I], F32, name="t1")
-            nc.vector.tensor_tensor(
-                out=t1_tiles[k][:],
-                in0=dsw[:, k * SC * I : (k + 1) * SC * I].rearrange("p (t i) -> p t i", i=I),
-                in1=gsb_tiles[k][:].unsqueeze(2).to_broadcast([P, SC, I]),
-                op=ALU.mult,
-            )
+            for tl in range(SC):
+                c0 = (k * SC + tl) * I
+                nc.scalar.activation(
+                    out=t1_tiles[k][:, tl, :], in_=dsw[:, c0 : c0 + I], func=ACT.Copy,
+                    scale=gsb_tiles[k][:, tl : tl + 1],
+                )
 
         def finish(k, half):
             n = SC * I // 2
@@ -314,21 +322,40 @@ def tile_bsplinekanlayer_t_kernel(tc, x, spline_parameters, w_b, w_s, grad_out, 
             nc.sync.dma_start(out=out_view[:, c0 : c0 + n], in_=o_c[:])
 
         transposes(0)
-        for j in range(10):
-            abs_instr(0, j)
+        for j in range(NJ):
+            abs_instr(0, j, 0, GT)
         copy_out(0, 0)
         copy_out(0, 1)
-        for j in range(10, NJ):
-            abs_instr(0, j)
+        for j in range(NJ):
+            abs_instr(0, j, GT, CH)
         quantise(0)
         nc.vector.tensor_scalar(out=hwb[:], in0=wb_raw[:], scalar1=0.5, scalar2=None, op0=ALU.mult)
         nc.vector.tensor_scalar(out=nqwb[:], in0=wb_raw[:], scalar1=-0.25, scalar2=None, op0=ALU.mult)
         nc.vector.tensor_scalar(out=pqwb[:], in0=wb_raw[:], scalar1=0.25, scalar2=None, op0=ALU.mult)
         nc.vector.tensor_scalar(out=wsn[:], in0=ws_raw[:], scalar1=-INV_H, scalar2=None, op0=ALU.mult)
 
-        finish_at = {7: 0, 9: 1, 12: 2}
+        unary_at = {}
+        it = 0
+        for n in range(16):
+            unary_at[n] = it
+            if n % 3 != 0:
+                it += 1
+        mult_at = {}
+        add_at = {}
+        silu_at = {}
+        finish_at = {}
+        for k in range(4):
+            mult_at[k] = unary_at[4 * k + 2] + 1
+            add_at[k] = max(mult_at[k], unary_at[4 * k + 3]) + 1
+            silu_at[k] = max(add_at[k] + 1, 4 * k + 4)
+            first = max(silu_at[k] + 1, 4 * k + 5)
+            if k > 0:
+                first = max(first, finish_at[(k - 1, 1)] + 1)
+            finish_at[(k, 0)] = first
+            finish_at[(k, 1)] = first + 1
 
         for gi in range(NG):
+            final = gi == NG - 1
             if gi + G_BUFS < NG:
                 load_g(gi + G_BUFS)
             c_next = gi // 2 + 1
@@ -352,27 +379,44 @@ def tile_bsplinekanlayer_t_kernel(tc, x, spline_parameters, w_b, w_s, grad_out, 
                 g1s = sums_to_rows_a(gi // 4)
             for j in fill[5:]:
                 abs_instr(c_next, j)
-            if 1 <= gi <= 4:
-                dsilu_scalar(gi - 1)
+            for n in range(16):
+                if unary_at[n] == gi:
+                    dsilu_scalar(n // 4, n % 4)
+            for k in range(3):
+                if silu_at[k] == gi:
+                    silu_term(k)
             for t4 in range(GT):
                 mx_tile(gi, t4)
                 if t4 == 1:
                     if nxt < NG:
                         quantise(nxt)
+                    if final:
+                        for half in (256, 128, 64, 32):
+                            halve(nc.gpsimd, gi, 0, 2, half)
+                    else:
+                        halve(nc.vector, gi, 0, 2, 256)
                     if gi % 4 == 3:
                         sums_to_rows_b(gi // 4, g1s)
-                if t4 == 2 and gi == NG - 1:
-                    silu_term(3)
+                    if final:
+                        silu_term(3)
+                if t4 == 2 and final:
                     finish(3, 0)
-            halve(nc.vector, gi, 0, 4, 256)
-            for half in (128, 64, 32):
-                halve(nc.vector, gi, 0, 4, half)
-            last_add(nc.vector, gi, 0, 4)
-            if 5 <= gi <= 8:
-                dsilu_vector(gi - 5)
-            if gi in finish_at:
-                k = finish_at[gi]
-                silu_term(k)
-                finish(k, 0)
-                finish(k, 1)
+            if not final:
+                halve(nc.vector, gi, 2, 4, 256)
+                for half in (128, 64, 32):
+                    halve(nc.gpsimd, gi, 0, 4, half)
+                last_add(nc.gpsimd, gi, 0, 4)
+            else:
+                for half in (256, 128, 64, 32):
+                    halve(nc.vector, gi, 2, 4, half)
+                last_add(nc.vector, gi, 0, 4)
+            for k in range(4):
+                if mult_at[k] == gi:
+                    dsilu_mult(k)
+                if add_at[k] == gi:
+                    dsilu_add(k)
+            for k in range(3):
+                for half in range(2):
+                    if finish_at[(k, half)] == gi:
+                        finish(k, half)
         finish(3, 1)

@@ -25,8 +25,6 @@ SC = 16
 NG = NT // GT
 INV_H = 57.0 / 7.0
 G_BUFS = 6
-BSTEP = 64
-LAST0 = (GT - 1) * BSTEP
 
 FLOPS = 2 * B * O * I * K
 
@@ -42,7 +40,7 @@ def tile_bsplinekanlayer_t_kernel(tc, x, spline_parameters, w_b, w_s, grad_out, 
         rpool = ctx.enter_context(tc.tile_pool(name="rpool", bufs=4))
         small = ctx.enter_context(tc.tile_pool(name="small", bufs=2))
         ps_tp = ctx.enter_context(tc.psum_pool(name="ps_tp", bufs=2))
-        ps_a = ctx.enter_context(tc.psum_pool(name="ps_a", bufs=4))
+        ps_a = ctx.enter_context(tc.psum_pool(name="ps_a", bufs=3))
         ps_b = ctx.enter_context(tc.psum_pool(name="ps_b", bufs=1))
         ps_g = ctx.enter_context(tc.psum_pool(name="ps_g", bufs=1))
         ctx.enter_context(tc.manual_schedule())
@@ -102,8 +100,8 @@ def tile_bsplinekanlayer_t_kernel(tc, x, spline_parameters, w_b, w_s, grad_out, 
         pos = const.tile([P, 4 * O], BF16, align_bytes=64)
         neg = const.tile([P, 4 * O], BF16, align_bytes=64)
         last = const.tile([P, 4 * I], BF16, align_bytes=64)
-        cl = const.tile([P, 2 * O], U32, align_bytes=64)
-        sl = const.tile([P, 2 * O], U8, align_bytes=64)
+        cl = const.tile([P, P], U32, align_bytes=64)
+        sl = const.tile([P, P], U8, align_bytes=64)
         nc.vector.memset(cl[:].bitcast(I32), 0)
         nc.vector.memset(sl[:].bitcast(I32), 0)
         nc.gpsimd.memset(neg[:, 0 : 4 * I], 0.0)
@@ -133,7 +131,7 @@ def tile_bsplinekanlayer_t_kernel(tc, x, spline_parameters, w_b, w_s, grad_out, 
         nc.vector.quantize_mx(out=c1[:].bitcast(E4X4), scales=s1[:], in_=pos[:])
         nc.vector.quantize_mx(out=cn[:].bitcast(E4X4), scales=sn[:], in_=neg[:])
         nc.vector.quantize_mx(
-            out=cl[:, LAST0 : LAST0 + I].bitcast(E4X4), scales=sl[:, LAST0 : LAST0 + I], in_=last[:]
+            out=cl[:, 0:I].bitcast(E4X4), scales=sl[:, 0:I], in_=last[:]
         )
 
         def abs_instr(c, j, lo=0, hi=CH):
@@ -207,14 +205,6 @@ def tile_bsplinekanlayer_t_kernel(tc, x, spline_parameters, w_b, w_s, grad_out, 
                 rhs=cn[:].bitcast(E4X4), rhs_scale=sn[:], start=False, stop=True,
             )
             if t4 == 0:
-                bank_b[gi] = ps_b.tile([P, O], F32, name="bank_b")
-            w0 = LAST0 - BSTEP * t4
-            nc.tensor.matmul_mx(
-                out=bank_b[gi][:], lhsT=lhs, lhsT_scale=lhs_s,
-                rhs=cl[:, w0 : w0 + O].bitcast(E4X4), rhs_scale=sl[:, w0 : w0 + O],
-                start=(t4 == 0), stop=(t4 == GT - 1),
-            )
-            if t4 == 0:
                 p_tiles[gi] = ppool.tile([P, GT, W], F32, name="p_t")
             tile_no = gi * GT + t4
             t_tile = t_tiles[tile_no // CH]
@@ -223,14 +213,37 @@ def tile_bsplinekanlayer_t_kernel(tc, x, spline_parameters, w_b, w_s, grad_out, 
                 out=p_tiles[gi][:, t4, 0:O], in0=t_tile[:, tl, 0:O], scalar=1.0, in1=bank_a[:],
                 op0=ALU.min, op1=ALU.mult,
             )
-            if t4 == GT - 1:
-                nc.vector.scalar_tensor_tensor(
-                    out=p_tiles[gi][:, :, O:W],
-                    in0=t_tile[:, tl - (GT - 1) : tl + 1, O:W],
-                    scalar=1.0,
-                    in1=bank_b[gi][:, 0 : GT * BSTEP].rearrange("p (t c) -> p t c", c=BSTEP)[:, :, 0:I],
-                    op0=ALU.min, op1=ALU.mult,
-                )
+
+        bank_t = {}
+        d16t = {}
+
+        def last_pass(gi):
+            bank_t[gi] = ps_b.tile([P, O], F32, name="bank_t")
+            nc.tensor.matmul_mx(
+                out=bank_t[gi][:], lhsT=cl[:].bitcast(E4X4), lhsT_scale=sl[:],
+                rhs=gcode[gi][:].bitcast(E5X4), rhs_scale=gscale[gi][:], start=True, stop=True,
+            )
+
+        def last_out(gi):
+            d16t[gi] = small.tile([P, O], F32, name="d16t")
+            nc.scalar.copy(out=d16t[gi][:], in_=bank_t[gi][:])
+
+        def last_back(gi):
+            bank_b[gi] = ps_b.tile([P, GT, P], F32, name="bank_b")
+            for t4 in range(GT):
+                nc.tensor.transpose(bank_b[gi][:, t4, :], d16t[gi][:, P * t4 : P * t4 + P], ident[:])
+
+        def last_product(gi):
+            tile_no = gi * GT
+            t_tile = t_tiles[tile_no // CH]
+            tl = tile_no % CH
+            nc.vector.scalar_tensor_tensor(
+                out=p_tiles[gi][:, :, O:W],
+                in0=t_tile[:, tl : tl + GT, O:W],
+                scalar=1.0,
+                in1=bank_b[gi][:, :, 0:I],
+                op0=ALU.min, op1=ALU.mult,
+            )
 
         def r_slice(gi, first, count):
             k = gi // 4
@@ -365,6 +378,12 @@ def tile_bsplinekanlayer_t_kernel(tc, x, spline_parameters, w_b, w_s, grad_out, 
             nxt = gi + 1
             if nxt < NG:
                 transposes(nxt)
+            if gi > 0:
+                last_back(gi - 1)
+                last_product(gi - 1)
+                for half in (128, 64, 32):
+                    halve(nc.gpsimd, gi - 1, 0, 4, half)
+                last_add(nc.gpsimd, gi - 1, 0, 4)
             for j in fill[0:3]:
                 abs_instr(c_next, j)
             if nxt < NG:
@@ -374,6 +393,8 @@ def tile_bsplinekanlayer_t_kernel(tc, x, spline_parameters, w_b, w_s, grad_out, 
             if nxt < NG:
                 copy_out(nxt, 1)
             row_sums(gi)
+            last_pass(gi)
+            last_out(gi)
             g1s = None
             if gi % 4 == 3:
                 g1s = sums_to_rows_a(gi // 4)
@@ -399,14 +420,13 @@ def tile_bsplinekanlayer_t_kernel(tc, x, spline_parameters, w_b, w_s, grad_out, 
                         sums_to_rows_b(gi // 4, g1s)
                     if final:
                         silu_term(3)
+                        last_back(gi)
                 if t4 == 2 and final:
                     finish(3, 0)
             if not final:
                 halve(nc.vector, gi, 2, 4, 256)
-                for half in (128, 64, 32):
-                    halve(nc.gpsimd, gi, 0, 4, half)
-                last_add(nc.gpsimd, gi, 0, 4)
             else:
+                last_product(gi)
                 for half in (256, 128, 64, 32):
                     halve(nc.vector, gi, 2, 4, half)
                 last_add(nc.vector, gi, 0, 4)

@@ -42,7 +42,7 @@ def tile_bsplinekanlayer_t_kernel(tc, x, spline_parameters, w_b, w_s, grad_out, 
         ps_tp = ctx.enter_context(tc.psum_pool(name="ps_tp", bufs=2))
         ps_a = ctx.enter_context(tc.psum_pool(name="ps_a", bufs=3))
         ps_b = ctx.enter_context(tc.psum_pool(name="ps_b", bufs=1))
-        ps_g = ctx.enter_context(tc.psum_pool(name="ps_g", bufs=1))
+        ps_m = ctx.enter_context(tc.psum_pool(name="ps_m", bufs=1))
         ctx.enter_context(tc.manual_schedule())
 
         g_view = grad_out.rearrange("(p t) o -> p (t o)", t=NT)
@@ -54,8 +54,7 @@ def tile_bsplinekanlayer_t_kernel(tc, x, spline_parameters, w_b, w_s, grad_out, 
         gscale = {}
         t_tiles = {}
         p_tiles = {}
-        r_tiles = {}
-        g1_tiles = {}
+        acc_sb = {}
         gsb_tiles = {}
         t1_tiles = {}
 
@@ -96,6 +95,10 @@ def tile_bsplinekanlayer_t_kernel(tc, x, spline_parameters, w_b, w_s, grad_out, 
         )
         for h in range(4):
             nc.vector.tensor_copy(out=sel[:, h, 32 * h : 32 * h + 32], in_=a32[:])
+
+        misc = ps_m.tile([P, O], F32, name="misc")
+        r_all = ps_m.tile([P, O], F32, name="r_all")
+        acc = misc[:, P : 2 * P]
 
         pos = const.tile([P, 4 * O], BF16, align_bytes=64)
         neg = const.tile([P, 4 * O], BF16, align_bytes=64)
@@ -174,15 +177,12 @@ def tile_bsplinekanlayer_t_kernel(tc, x, spline_parameters, w_b, w_s, grad_out, 
             )
 
         def row_sums(gi):
-            k = gi // 4
-            if gi % 4 == 0:
-                g1_tiles[k] = ps_g.tile([P, 5 * SC], F32, name="g1")
             for t4 in range(GT):
                 tl = (gi % 4) * GT + t4
                 for h in range(4):
                     col = h * SC + tl
                     nc.tensor.matmul(
-                        out=g1_tiles[k][:, col : col + 1],
+                        out=misc[:, col : col + 1],
                         lhsT=grp[gi][:, O * t4 + P * h : O * t4 + P * h + P],
                         rhs=ones[:, 0:1],
                         start=True,
@@ -205,12 +205,15 @@ def tile_bsplinekanlayer_t_kernel(tc, x, spline_parameters, w_b, w_s, grad_out, 
                 rhs=cn[:].bitcast(E4X4), rhs_scale=sn[:], start=False, stop=True,
             )
             if t4 == 0:
-                p_tiles[gi] = ppool.tile([P, GT, W], F32, name="p_t")
+                p_tiles[gi] = ppool.tile([P, NJ, GT, I], F32, name="p_t")
             tile_no = gi * GT + t4
             t_tile = t_tiles[tile_no // CH]
             tl = tile_no % CH
             nc.vector.scalar_tensor_tensor(
-                out=p_tiles[gi][:, t4, 0:O], in0=t_tile[:, tl, 0:O], scalar=1.0, in1=bank_a[:],
+                out=p_tiles[gi][:, 0:K, t4, :],
+                in0=t_tile[:, tl, 0:O].rearrange("p (j i) -> p j i", i=I),
+                scalar=1.0,
+                in1=bank_a[:].rearrange("p (j i) -> p j i", i=I),
                 op0=ALU.min, op1=ALU.mult,
             )
 
@@ -218,7 +221,7 @@ def tile_bsplinekanlayer_t_kernel(tc, x, spline_parameters, w_b, w_s, grad_out, 
         d16t = {}
 
         def last_pass(gi):
-            bank_t[gi] = ps_b.tile([P, O], F32, name="bank_t")
+            bank_t[gi] = ps_b.tile([P, O], F32, name="bank_tb")
             nc.tensor.matmul_mx(
                 out=bank_t[gi][:], lhsT=cl[:].bitcast(E4X4), lhsT_scale=sl[:],
                 rhs=gcode[gi][:].bitcast(E5X4), rhs_scale=gscale[gi][:], start=True, stop=True,
@@ -229,7 +232,7 @@ def tile_bsplinekanlayer_t_kernel(tc, x, spline_parameters, w_b, w_s, grad_out, 
             nc.scalar.copy(out=d16t[gi][:], in_=bank_t[gi][:])
 
         def last_back(gi):
-            bank_b[gi] = ps_b.tile([P, GT, P], F32, name="bank_b")
+            bank_b[gi] = ps_b.tile([P, GT, P], F32, name="bank_tb")
             for t4 in range(GT):
                 nc.tensor.transpose(bank_b[gi][:, t4, :], d16t[gi][:, P * t4 : P * t4 + P], ident[:])
 
@@ -238,32 +241,36 @@ def tile_bsplinekanlayer_t_kernel(tc, x, spline_parameters, w_b, w_s, grad_out, 
             t_tile = t_tiles[tile_no // CH]
             tl = tile_no % CH
             nc.vector.scalar_tensor_tensor(
-                out=p_tiles[gi][:, :, O:W],
+                out=p_tiles[gi][:, K, :, :],
                 in0=t_tile[:, tl : tl + GT, O:W],
                 scalar=1.0,
                 in1=bank_b[gi][:, :, 0:I],
                 op0=ALU.min, op1=ALU.mult,
             )
 
-        def r_slice(gi, first, count):
-            k = gi // 4
-            if k not in r_tiles:
-                r_tiles[k] = rpool.tile([P, SC * I], F32, name="r_k")
-            col = ((gi % 4) * GT + first) * I
-            return r_tiles[k][:, col : col + count * I].rearrange("p (t i) -> p t i", i=I)
-
-        def halve(eng, gi, t0, t1, half):
-            p_t = p_tiles[gi]
-            eng.tensor_tensor(
-                out=p_t[:, t0:t1, 0:half], in0=p_t[:, t0:t1, 0:half], in1=p_t[:, t0:t1, half : 2 * half],
-                op=ALU.add,
+        def halve(gi, t0, t1):
+            p_v = p_tiles[gi][:].rearrange("p j t i -> p j (t i)")
+            nc.vector.tensor_tensor(
+                out=p_v[:, 0:8, I * t0 : I * t1], in0=p_v[:, 0:8, I * t0 : I * t1],
+                in1=p_v[:, 8:16, I * t0 : I * t1], op=ALU.add,
             )
 
-        def last_add(eng, gi, t0, t1):
-            p_t = p_tiles[gi]
-            eng.tensor_tensor(
-                out=r_slice(gi, t0, t1 - t0), in0=p_t[:, t0:t1, 0:I], in1=p_t[:, t0:t1, O:W], op=ALU.add
-            )
+        def reduce_group(gi):
+            p_v = p_tiles[gi][:].rearrange("p j t i -> p j (t i)")
+            slabs = list(range(8)) + [K]
+            for n, j in enumerate(slabs):
+                nc.tensor.matmul(
+                    out=acc, lhsT=p_v[:, j, :], rhs=ident[:], is_transpose=True,
+                    start=(n == 0), stop=(n == len(slabs) - 1),
+                )
+
+        def acc_copy(gi):
+            acc_sb[gi] = small.tile([P, P], F32, name="acc_sb")
+            nc.vector.tensor_copy(out=acc_sb[gi][:], in_=acc)
+
+        def turn_back(gi):
+            col = (gi % 4) * P
+            nc.tensor.transpose(r_all[:, col : col + P], acc_sb[gi][:], ident[:])
 
         th = const.tile([P, NT * I], F32)
         q = const.tile([P, NT * I], F32)
@@ -274,58 +281,58 @@ def tile_bsplinekanlayer_t_kernel(tc, x, spline_parameters, w_b, w_s, grad_out, 
         wsn = const.tile([P, 1], F32)
         HALF = NT * I // 2
 
-        def dsilu_scalar(k, step):
+        def dsilu_tanh(k):
+            cs = slice(k * SC * I, (k + 1) * SC * I)
+            nc.scalar.activation(out=th[:, cs], in_=x_sb[:, cs], func=ACT.Tanh, scale=0.5)
+
+        def dsilu_pool(k, step):
             cs = slice(k * SC * I, (k + 1) * SC * I)
             if step == 0:
-                nc.scalar.activation(out=th[:, cs], in_=x_sb[:, cs], func=ACT.Tanh, scale=0.5)
+                nc.gpsimd.tensor_tensor(out=q[:, cs], in0=th[:, cs], in1=th[:, cs], op=ALU.mult)
             elif step == 1:
-                nc.scalar.activation(out=q[:, cs], in_=th[:, cs], func=ACT.Square)
+                nc.gpsimd.tensor_scalar(
+                    out=q[:, cs], in0=q[:, cs], scalar1=nqwb[:, 0:1], scalar2=pqwb[:, 0:1],
+                    op0=ALU.mult, op1=ALU.add,
+                )
             elif step == 2:
-                nc.scalar.activation(
-                    out=q[:, cs], in_=q[:, cs], func=ACT.Identity, scale=nqwb[:, 0:1], bias=pqwb[:, 0:1]
+                nc.gpsimd.tensor_tensor(out=q[:, cs], in0=q[:, cs], in1=x_sb[:, cs], op=ALU.mult)
+            elif step == 3:
+                nc.gpsimd.tensor_scalar(
+                    out=th[:, cs], in0=th[:, cs], scalar1=hwb[:, 0:1], scalar2=hwb[:, 0:1],
+                    op0=ALU.mult, op1=ALU.add,
                 )
             else:
-                nc.scalar.activation(
-                    out=th[:, cs], in_=th[:, cs], func=ACT.Identity, scale=hwb[:, 0:1], bias=hwb[:, 0:1]
-                )
-
-        def dsilu_mult(k):
-            cs = slice(k * SC * I, (k + 1) * SC * I)
-            nc.gpsimd.tensor_tensor(out=q[:, cs], in0=q[:, cs], in1=x_sb[:, cs], op=ALU.mult)
-
-        def dsilu_add(k):
-            cs = slice(k * SC * I, (k + 1) * SC * I)
-            nc.vector.tensor_tensor(out=dsw[:, cs], in0=q[:, cs], in1=th[:, cs], op=ALU.add)
+                nc.gpsimd.tensor_tensor(out=dsw[:, cs], in0=q[:, cs], in1=th[:, cs], op=ALU.add)
 
         def sums_to_rows_a(k):
             g1s = small.tile([P, 4 * SC], F32, name="g1s")
-            nc.scalar.copy(out=g1s[:], in_=g1_tiles[k][:, 0 : 4 * SC])
+            nc.scalar.copy(out=g1s[:], in_=misc[:, 0 : 4 * SC])
             return g1s
 
         def sums_to_rows_b(k, g1s):
             for h in range(4):
                 nc.tensor.matmul(
-                    out=g1_tiles[k][:, 4 * SC : 5 * SC], lhsT=sel[:, h, :],
+                    out=misc[:, 4 * SC : 5 * SC], lhsT=sel[:, h, :],
                     rhs=g1s[:, h * SC : (h + 1) * SC], start=(h == 0), stop=(h == 3),
                 )
             gsb_tiles[k] = rpool.tile([P, SC], F32, name="gsb")
-            nc.scalar.copy(out=gsb_tiles[k][:], in_=g1_tiles[k][:, 4 * SC : 5 * SC])
+            nc.scalar.copy(out=gsb_tiles[k][:], in_=misc[:, 4 * SC : 5 * SC])
 
         def silu_term(k):
             t1_tiles[k] = small.tile([P, SC, I], F32, name="t1")
-            for tl in range(SC):
-                c0 = (k * SC + tl) * I
-                nc.scalar.activation(
-                    out=t1_tiles[k][:, tl, :], in_=dsw[:, c0 : c0 + I], func=ACT.Copy,
-                    scale=gsb_tiles[k][:, tl : tl + 1],
-                )
+            nc.gpsimd.tensor_tensor(
+                out=t1_tiles[k][:],
+                in0=dsw[:, k * SC * I : (k + 1) * SC * I].rearrange("p (t i) -> p t i", i=I),
+                in1=gsb_tiles[k][:].unsqueeze(2).to_broadcast([P, SC, I]),
+                op=ALU.mult,
+            )
 
         def finish(k, half):
             n = SC * I // 2
             o_c = small.tile([P, n], F32, name="o_c")
             nc.vector.scalar_tensor_tensor(
                 out=o_c[:],
-                in0=r_tiles[k][:, half * n : (half + 1) * n],
+                in0=r_all[:, half * n : (half + 1) * n],
                 scalar=wsn[:, 0:1],
                 in1=t1_tiles[k][:].rearrange("p t i -> p (t i)")[:, half * n : (half + 1) * n],
                 op0=ALU.mult,
@@ -347,43 +354,41 @@ def tile_bsplinekanlayer_t_kernel(tc, x, spline_parameters, w_b, w_s, grad_out, 
         nc.vector.tensor_scalar(out=pqwb[:], in0=wb_raw[:], scalar1=0.25, scalar2=None, op0=ALU.mult)
         nc.vector.tensor_scalar(out=wsn[:], in0=ws_raw[:], scalar1=-INV_H, scalar2=None, op0=ALU.mult)
 
-        unary_at = {}
-        it = 0
-        for n in range(16):
-            unary_at[n] = it
-            if n % 3 != 0:
-                it += 1
-        mult_at = {}
-        add_at = {}
-        silu_at = {}
-        finish_at = {}
+        tanh_at = {}
+        pool_at = {}
         for k in range(4):
-            mult_at[k] = unary_at[4 * k + 2] + 1
-            add_at[k] = max(mult_at[k], unary_at[4 * k + 3]) + 1
-            silu_at[k] = max(add_at[k] + 1, 4 * k + 4)
-            first = max(silu_at[k] + 1, 4 * k + 5)
-            if k > 0:
-                first = max(first, finish_at[(k - 1, 1)] + 1)
-            finish_at[(k, 0)] = first
-            finish_at[(k, 1)] = first + 1
+            tanh_at[k] = 3 * k + 1
+            for step in range(5):
+                pool_at[(k, step)] = 3 * k + 1 + step // 2
 
-        for gi in range(NG):
-            final = gi == NG - 1
+        for gi in range(NG + 3):
+            live = gi < NG
+            nxt = gi + 1
             if gi + G_BUFS < NG:
                 load_g(gi + G_BUFS)
             c_next = gi // 2 + 1
             fill = []
             if c_next < NT // CH:
                 fill = list(range(0, 9)) if gi % 2 == 0 else list(range(9, NJ))
-            nxt = gi + 1
             if nxt < NG:
                 transposes(nxt)
-            if gi > 0:
+            if 0 <= gi - 2 < NG:
+                reduce_group(gi - 2)
+            if 0 <= gi - 3 < NG:
+                turn_back(gi - 3)
+            if 1 <= gi <= NG:
                 last_back(gi - 1)
+            if live:
+                row_sums(gi)
+            if 1 <= gi <= NG:
                 last_product(gi - 1)
-                for half in (128, 64, 32):
-                    halve(nc.gpsimd, gi - 1, 0, 4, half)
-                last_add(nc.gpsimd, gi - 1, 0, 4)
+            if 0 <= gi - 2 < NG:
+                acc_copy(gi - 2)
+            for k in range(4):
+                if gi == 4 * k + 4:
+                    finish(k, 0)
+                if gi == 4 * k + 6:
+                    finish(k, 1)
             for j in fill[0:3]:
                 abs_instr(c_next, j)
             if nxt < NG:
@@ -392,51 +397,30 @@ def tile_bsplinekanlayer_t_kernel(tc, x, spline_parameters, w_b, w_s, grad_out, 
                 abs_instr(c_next, j)
             if nxt < NG:
                 copy_out(nxt, 1)
-            row_sums(gi)
-            last_pass(gi)
-            last_out(gi)
+            if not live:
+                continue
             g1s = None
             if gi % 4 == 3:
                 g1s = sums_to_rows_a(gi // 4)
             for j in fill[5:]:
                 abs_instr(c_next, j)
-            for n in range(16):
-                if unary_at[n] == gi:
-                    dsilu_scalar(n // 4, n % 4)
-            for k in range(3):
-                if silu_at[k] == gi:
-                    silu_term(k)
+            for k in range(4):
+                if tanh_at[k] == gi:
+                    dsilu_tanh(k)
             for t4 in range(GT):
                 mx_tile(gi, t4)
                 if t4 == 1:
+                    last_pass(gi)
+                    last_out(gi)
                     if nxt < NG:
                         quantise(nxt)
-                    if final:
-                        for half in (256, 128, 64, 32):
-                            halve(nc.gpsimd, gi, 0, 2, half)
-                    else:
-                        halve(nc.vector, gi, 0, 2, 256)
+                    halve(gi, 0, 2)
                     if gi % 4 == 3:
                         sums_to_rows_b(gi // 4, g1s)
-                    if final:
-                        silu_term(3)
-                        last_back(gi)
-                if t4 == 2 and final:
-                    finish(3, 0)
-            if not final:
-                halve(nc.vector, gi, 2, 4, 256)
-            else:
-                last_product(gi)
-                for half in (256, 128, 64, 32):
-                    halve(nc.vector, gi, 2, 4, half)
-                last_add(nc.vector, gi, 0, 4)
+            halve(gi, 2, 4)
             for k in range(4):
-                if mult_at[k] == gi:
-                    dsilu_mult(k)
-                if add_at[k] == gi:
-                    dsilu_add(k)
-            for k in range(3):
-                for half in range(2):
-                    if finish_at[(k, half)] == gi:
-                        finish(k, half)
-        finish(3, 1)
+                for step in range(5):
+                    if pool_at[(k, step)] == gi:
+                        dsilu_pool(k, step)
+                if gi == 4 * k + 3:
+                    silu_term(k)

@@ -17,12 +17,12 @@ AX = mybir.AxisListType
 P = 128
 B, I, O, K = 8192, 32, 512, 16
 NT = B // P
-NJ = K + 1
-W = NJ * I
 GT = 4
+GS = 4
 CH = 8
-SC = 16
+SC = GT * GS
 NG = NT // GT
+NS = NT // SC
 INV_H = 57.0 / 7.0
 G_BUFS = 6
 
@@ -35,13 +35,12 @@ def tile_bsplinekanlayer_t_kernel(tc, x, spline_parameters, w_b, w_s, grad_out, 
         const = ctx.enter_context(tc.tile_pool(name="const", bufs=1))
         gpool = ctx.enter_context(tc.tile_pool(name="gpool", bufs=G_BUFS))
         grpool = ctx.enter_context(tc.tile_pool(name="grpool", bufs=3))
-        tpool = ctx.enter_context(tc.tile_pool(name="tpool", bufs=4))
+        cpool = ctx.enter_context(tc.tile_pool(name="cpool", bufs=2))
+        tpool = ctx.enter_context(tc.tile_pool(name="tpool", bufs=3))
         ppool = ctx.enter_context(tc.tile_pool(name="ppool", bufs=4))
-        rpool = ctx.enter_context(tc.tile_pool(name="rpool", bufs=4))
         small = ctx.enter_context(tc.tile_pool(name="small", bufs=2))
         ps_tp = ctx.enter_context(tc.psum_pool(name="ps_tp", bufs=2))
         ps_a = ctx.enter_context(tc.psum_pool(name="ps_a", bufs=3))
-        ps_b = ctx.enter_context(tc.psum_pool(name="ps_b", bufs=1))
         ps_m = ctx.enter_context(tc.psum_pool(name="ps_m", bufs=1))
         ctx.enter_context(tc.manual_schedule())
 
@@ -54,7 +53,14 @@ def tile_bsplinekanlayer_t_kernel(tc, x, spline_parameters, w_b, w_s, grad_out, 
         gscale = {}
         t_tiles = {}
         p_tiles = {}
-        acc_sb = {}
+        tp_tiles = {}
+        acc_t = {}
+        x_t = {}
+        m16 = {}
+        b16 = {}
+        p16 = {}
+        sum_sb = {}
+        r_bank = {}
         gsb_tiles = {}
         t1_tiles = {}
 
@@ -85,6 +91,8 @@ def tile_bsplinekanlayer_t_kernel(tc, x, spline_parameters, w_b, w_s, grad_out, 
 
         ident = const.tile([P, P], F32)
         make_identity(nc, ident[:])
+        ident_bf = const.tile([P, P], BF16)
+        make_identity(nc, ident_bf[:])
         ones = const.tile([P, 2], BF16)
         nc.vector.memset(ones[:], 1.0)
         sel = const.tile([P, 4, P], F32)
@@ -95,18 +103,10 @@ def tile_bsplinekanlayer_t_kernel(tc, x, spline_parameters, w_b, w_s, grad_out, 
         )
         for h in range(4):
             nc.vector.tensor_copy(out=sel[:, h, 32 * h : 32 * h + 32], in_=a32[:])
-
-        misc = ps_m.tile([P, O], F32, name="misc")
-        r_all = ps_m.tile([P, O], F32, name="r_all")
-        acc = misc[:, P : 2 * P]
+        g1 = ps_m.tile([P, 5 * SC], F32, name="g1")
 
         pos = const.tile([P, 4 * O], BF16, align_bytes=64)
         neg = const.tile([P, 4 * O], BF16, align_bytes=64)
-        last = const.tile([P, 4 * I], BF16, align_bytes=64)
-        cl = const.tile([P, P], U32, align_bytes=64)
-        sl = const.tile([P, P], U8, align_bytes=64)
-        nc.vector.memset(cl[:].bitcast(I32), 0)
-        nc.vector.memset(sl[:].bitcast(I32), 0)
         nc.gpsimd.memset(neg[:, 0 : 4 * I], 0.0)
         p_perm = praw[:].rearrange("p t (i k) -> p k i t", k=K)
         nc.vector.tensor_copy(
@@ -120,26 +120,34 @@ def tile_bsplinekanlayer_t_kernel(tc, x, spline_parameters, w_b, w_s, grad_out, 
             op0=ALU.mult,
             op1=ALU.add,
         )
-        nc.vector.tensor_scalar(
-            out=last[:].rearrange("p (i t) -> p i t", t=4),
-            in0=p_perm[:, K - 1],
-            scalar1=-1.0,
-            scalar2=None,
-            op0=ALU.mult,
-        )
         c1 = const.tile([P, O], U32, align_bytes=64)
         s1 = const.tile([P, O], U8, align_bytes=64)
         cn = const.tile([P, O], U32, align_bytes=64)
         sn = const.tile([P, O], U8, align_bytes=64)
         nc.vector.quantize_mx(out=c1[:].bitcast(E4X4), scales=s1[:], in_=pos[:])
         nc.vector.quantize_mx(out=cn[:].bitcast(E4X4), scales=sn[:], in_=neg[:])
-        nc.vector.quantize_mx(
-            out=cl[:, 0:I].bitcast(E4X4), scales=sl[:, 0:I], in_=last[:]
-        )
+        zsrc = const.tile([P, GT, GT, 4 * I], BF16, align_bytes=64)
+        zc = const.tile([P, GT * P], U32, align_bytes=64)
+        zs = const.tile([P, GT * P], U8, align_bytes=64)
+        nc.gpsimd.memset(zsrc[:], 0.0)
+        for c in range(GT):
+            nc.gpsimd.tensor_scalar(
+                out=zsrc[:, c, c, :].rearrange("p (i t) -> p i t", t=4),
+                in0=p_perm[:, K - 1],
+                scalar1=-1.0,
+                scalar2=0.0,
+                op0=ALU.mult,
+                op1=ALU.add,
+            )
+
+        def quantise_z():
+            nc.vector.quantize_mx(
+                out=zc[:].bitcast(E4X4), scales=zs[:], in_=zsrc[:].rearrange("p a b w -> p (a b w)")
+            )
 
         def abs_instr(c, j, lo=0, hi=CH):
             if c not in t_tiles:
-                t_tiles[c] = tpool.tile([P, CH, W], F32, name="Tt")
+                t_tiles[c] = tpool.tile([P, CH, O], F32, name="Tt")
             nc.scalar.activation(
                 out=t_tiles[c][:, lo:hi, I * j : I * j + I],
                 in_=x3[:, c * CH + lo : c * CH + hi, :],
@@ -147,8 +155,6 @@ def tile_bsplinekanlayer_t_kernel(tc, x, spline_parameters, w_b, w_s, grad_out, 
                 scale=INV_H,
                 bias=float(8 - j),
             )
-
-        tp_tiles = {}
 
         def transposes(gi):
             gw = g_nat[gi][:].bitcast(F32)
@@ -170,31 +176,33 @@ def tile_bsplinekanlayer_t_kernel(tc, x, spline_parameters, w_b, w_s, grad_out, 
             )
 
         def quantise(gi):
-            gcode[gi] = grpool.tile([P, GT * P], U32, align_bytes=64, name="gc")
-            gscale[gi] = grpool.tile([P, GT * P], U8, align_bytes=64, name="gs")
-            nc.vector.quantize_mx(
-                out=gcode[gi][:].bitcast(E5X4), scales=gscale[gi][:], in_=grp[gi][:]
-            )
+            s, a = gi // GS, gi % GS
+            if a == 0:
+                gcode[s] = cpool.tile([P, GT, GS, P], U32, align_bytes=64, name="gc")
+                gscale[s] = cpool.tile([P, GT, GS, P], U8, align_bytes=64, name="gs")
+            for c in range(GT):
+                nc.vector.quantize_mx(
+                    out=gcode[s][:, c, a, :].bitcast(E5X4), scales=gscale[s][:, c, a, :],
+                    in_=grp[gi][:, O * c : O * c + O],
+                )
 
         def row_sums(gi):
             for t4 in range(GT):
-                tl = (gi % 4) * GT + t4
+                tl = (gi % GS) * GT + t4
                 for h in range(4):
                     col = h * SC + tl
                     nc.tensor.matmul(
-                        out=misc[:, col : col + 1],
+                        out=g1[:, col : col + 1],
                         lhsT=grp[gi][:, O * t4 + P * h : O * t4 + P * h + P],
                         rhs=ones[:, 0:1],
                         start=True,
                         stop=True,
                     )
 
-        bank_b = {}
-
-        def mx_tile(gi, t4):
-            cols = slice(P * t4, P * t4 + P)
-            lhs = gcode[gi][:, cols].bitcast(E5X4)
-            lhs_s = gscale[gi][:, cols]
+        def mx_tile(gi, c):
+            s, a = gi // GS, gi % GS
+            lhs = gcode[s][:, c, a, :].bitcast(E5X4)
+            lhs_s = gscale[s][:, c, a, :]
             bank_a = ps_a.tile([P, O], F32, name="bank_a")
             nc.tensor.matmul_mx(
                 out=bank_a[:], lhsT=lhs, lhsT_scale=lhs_s,
@@ -204,73 +212,76 @@ def tile_bsplinekanlayer_t_kernel(tc, x, spline_parameters, w_b, w_s, grad_out, 
                 out=bank_a[:], lhsT=lhs, lhsT_scale=lhs_s,
                 rhs=cn[:].bitcast(E4X4), rhs_scale=sn[:], start=False, stop=True,
             )
-            if t4 == 0:
-                p_tiles[gi] = ppool.tile([P, NJ, GT, I], F32, name="p_t")
-            tile_no = gi * GT + t4
-            t_tile = t_tiles[tile_no // CH]
-            tl = tile_no % CH
+            if c == 0:
+                p_tiles[gi] = ppool.tile([P, K, GT, I], F32, name="p_t")
+            tile_no = gi * GT + c
             nc.vector.scalar_tensor_tensor(
-                out=p_tiles[gi][:, 0:K, t4, :],
-                in0=t_tile[:, tl, 0:O].rearrange("p (j i) -> p j i", i=I),
+                out=p_tiles[gi][:, :, c, :],
+                in0=t_tiles[tile_no // CH][:, tile_no % CH, :].rearrange("p (j i) -> p j i", i=I),
                 scalar=1.0,
                 in1=bank_a[:].rearrange("p (j i) -> p j i", i=I),
                 op0=ALU.min, op1=ALU.mult,
             )
 
-        bank_t = {}
-        d16t = {}
-
-        def last_pass(gi):
-            bank_t[gi] = ps_b.tile([P, O], F32, name="bank_tb")
-            nc.tensor.matmul_mx(
-                out=bank_t[gi][:], lhsT=cl[:].bitcast(E4X4), lhsT_scale=sl[:],
-                rhs=gcode[gi][:].bitcast(E5X4), rhs_scale=gscale[gi][:], start=True, stop=True,
-            )
-
-        def last_out(gi):
-            d16t[gi] = small.tile([P, O], F32, name="d16t")
-            nc.scalar.copy(out=d16t[gi][:], in_=bank_t[gi][:])
-
-        def last_back(gi):
-            bank_b[gi] = ps_b.tile([P, GT, P], F32, name="bank_tb")
-            for t4 in range(GT):
-                nc.tensor.transpose(bank_b[gi][:, t4, :], d16t[gi][:, P * t4 : P * t4 + P], ident[:])
-
-        def last_product(gi):
-            tile_no = gi * GT
-            t_tile = t_tiles[tile_no // CH]
-            tl = tile_no % CH
-            nc.vector.scalar_tensor_tensor(
-                out=p_tiles[gi][:, K, :, :],
-                in0=t_tile[:, tl : tl + GT, O:W],
-                scalar=1.0,
-                in1=bank_b[gi][:, :, 0:I],
-                op0=ALU.min, op1=ALU.mult,
-            )
-
-        def halve(gi, t0, t1):
+        def halve(eng, gi, c0, c1_):
             p_v = p_tiles[gi][:].rearrange("p j t i -> p j (t i)")
-            nc.vector.tensor_tensor(
-                out=p_v[:, 0:8, I * t0 : I * t1], in0=p_v[:, 0:8, I * t0 : I * t1],
-                in1=p_v[:, 8:16, I * t0 : I * t1], op=ALU.add,
+            eng.tensor_tensor(
+                out=p_v[:, 0:8, I * c0 : I * c1_], in0=p_v[:, 0:8, I * c0 : I * c1_],
+                in1=p_v[:, 8:16, I * c0 : I * c1_], op=ALU.add,
             )
 
         def reduce_group(gi):
+            s, a = gi // GS, gi % GS
+            if a == 0:
+                acc_t[s] = ps_m.tile([P, GS * P], F32, name="acc_t")
             p_v = p_tiles[gi][:].rearrange("p j t i -> p j (t i)")
-            slabs = list(range(8)) + [K]
-            for n, j in enumerate(slabs):
+            for j in range(8):
                 nc.tensor.matmul(
-                    out=acc, lhsT=p_v[:, j, :], rhs=ident[:], is_transpose=True,
-                    start=(n == 0), stop=(n == len(slabs) - 1),
+                    out=acc_t[s][:, P * a : P * a + P], lhsT=p_v[:, j, :], rhs=ident[:], is_transpose=True,
+                    start=(j == 0), stop=(j == 7),
                 )
 
-        def acc_copy(gi):
-            acc_sb[gi] = small.tile([P, P], F32, name="acc_sb")
-            nc.vector.tensor_copy(out=acc_sb[gi][:], in_=acc)
+        def x_turn(s):
+            x_t[s] = ps_m.tile([P, GS, P], BF16, name="multi")
+            for a in range(GS):
+                col = (s * GS + a) * P
+                nc.tensor.transpose(x_t[s][:, a, :], x_sb[:, col : col + P], ident_bf[:])
 
-        def turn_back(gi):
-            col = (gi % 4) * P
-            nc.tensor.transpose(r_all[:, col : col + P], acc_sb[gi][:], ident[:])
+        def abs16(s):
+            m16[s] = small.tile([P, GS * P], F32, name="m16")
+            nc.scalar.activation(
+                out=m16[s][:], in_=x_t[s][:].rearrange("p a b -> p (a b)"), func=ACT.Abs,
+                scale=INV_H, bias=float(8 - K),
+            )
+
+        def last_pass(s):
+            b16[s] = ps_m.tile([P, GS * P], F32, name="multi")
+            for c in range(GT):
+                nc.tensor.matmul_mx(
+                    out=b16[s][:],
+                    lhsT=zc[:, P * c : P * c + P].bitcast(E4X4), lhsT_scale=zs[:, P * c : P * c + P],
+                    rhs=gcode[s][:, c, :, :].rearrange("p a b -> p (a b)").bitcast(E5X4),
+                    rhs_scale=gscale[s][:, c, :, :].rearrange("p a b -> p (a b)"),
+                    start=(c == 0), stop=(c == GT - 1),
+                )
+
+        def last_product(s):
+            p16[s] = small.tile([P, GS * P], F32, name="p16")
+            nc.vector.scalar_tensor_tensor(
+                out=p16[s][:], in0=m16[s][:], scalar=1.0, in1=b16[s][:], op0=ALU.min, op1=ALU.mult,
+            )
+
+        def sum_t(s, a0, a1):
+            if s not in sum_sb:
+                sum_sb[s] = small.tile([P, GS * P], F32, name="sum_sb")
+            cs = slice(P * a0, P * a1)
+            nc.vector.tensor_tensor(out=sum_sb[s][:, cs], in0=acc_t[s][:, cs], in1=p16[s][:, cs], op=ALU.add)
+
+        def turn_back(s, a0, a1):
+            if s not in r_bank:
+                r_bank[s] = ps_m.tile([P, GS * P], F32, name="multi")
+            for a in range(a0, a1):
+                nc.tensor.transpose(r_bank[s][:, P * a : P * a + P], sum_sb[s][:, P * a : P * a + P], ident[:])
 
         th = const.tile([P, NT * I], F32)
         q = const.tile([P, NT * I], F32)
@@ -279,44 +290,42 @@ def tile_bsplinekanlayer_t_kernel(tc, x, spline_parameters, w_b, w_s, grad_out, 
         nqwb = const.tile([P, 1], F32)
         pqwb = const.tile([P, 1], F32)
         wsn = const.tile([P, 1], F32)
-        HALF = NT * I // 2
 
-        def dsilu_tanh(k):
+        def dsilu_scalar(k, step):
             cs = slice(k * SC * I, (k + 1) * SC * I)
-            nc.scalar.activation(out=th[:, cs], in_=x_sb[:, cs], func=ACT.Tanh, scale=0.5)
+            if step == 0:
+                nc.scalar.activation(out=th[:, cs], in_=x_sb[:, cs], func=ACT.Tanh, scale=0.5)
+            elif step == 1:
+                nc.scalar.activation(out=q[:, cs], in_=th[:, cs], func=ACT.Square)
+            elif step == 2:
+                nc.scalar.activation(
+                    out=q[:, cs], in_=q[:, cs], func=ACT.Identity, scale=nqwb[:, 0:1], bias=pqwb[:, 0:1]
+                )
+            else:
+                nc.scalar.activation(
+                    out=th[:, cs], in_=th[:, cs], func=ACT.Identity, scale=hwb[:, 0:1], bias=hwb[:, 0:1]
+                )
 
         def dsilu_pool(k, step):
             cs = slice(k * SC * I, (k + 1) * SC * I)
             if step == 0:
-                nc.gpsimd.tensor_tensor(out=q[:, cs], in0=th[:, cs], in1=th[:, cs], op=ALU.mult)
-            elif step == 1:
-                nc.gpsimd.tensor_scalar(
-                    out=q[:, cs], in0=q[:, cs], scalar1=nqwb[:, 0:1], scalar2=pqwb[:, 0:1],
-                    op0=ALU.mult, op1=ALU.add,
-                )
-            elif step == 2:
                 nc.gpsimd.tensor_tensor(out=q[:, cs], in0=q[:, cs], in1=x_sb[:, cs], op=ALU.mult)
-            elif step == 3:
-                nc.gpsimd.tensor_scalar(
-                    out=th[:, cs], in0=th[:, cs], scalar1=hwb[:, 0:1], scalar2=hwb[:, 0:1],
-                    op0=ALU.mult, op1=ALU.add,
-                )
             else:
                 nc.gpsimd.tensor_tensor(out=dsw[:, cs], in0=q[:, cs], in1=th[:, cs], op=ALU.add)
 
         def sums_to_rows_a(k):
             g1s = small.tile([P, 4 * SC], F32, name="g1s")
-            nc.scalar.copy(out=g1s[:], in_=misc[:, 0 : 4 * SC])
+            nc.scalar.copy(out=g1s[:], in_=g1[:, 0 : 4 * SC])
             return g1s
 
         def sums_to_rows_b(k, g1s):
             for h in range(4):
                 nc.tensor.matmul(
-                    out=misc[:, 4 * SC : 5 * SC], lhsT=sel[:, h, :],
+                    out=g1[:, 4 * SC : 5 * SC], lhsT=sel[:, h, :],
                     rhs=g1s[:, h * SC : (h + 1) * SC], start=(h == 0), stop=(h == 3),
                 )
-            gsb_tiles[k] = rpool.tile([P, SC], F32, name="gsb")
-            nc.scalar.copy(out=gsb_tiles[k][:], in_=misc[:, 4 * SC : 5 * SC])
+            gsb_tiles[k] = small.tile([P, SC], F32, name="gsb")
+            nc.scalar.copy(out=gsb_tiles[k][:], in_=g1[:, 4 * SC : 5 * SC])
 
         def silu_term(k):
             t1_tiles[k] = small.tile([P, SC, I], F32, name="t1")
@@ -327,26 +336,26 @@ def tile_bsplinekanlayer_t_kernel(tc, x, spline_parameters, w_b, w_s, grad_out, 
                 op=ALU.mult,
             )
 
-        def finish(k, half):
-            n = SC * I // 2
-            o_c = small.tile([P, n], F32, name="o_c")
+        def finish(s, a0, a1):
+            n = (a1 - a0) * P
+            o_c = small.tile([P, GS * P], F32, name="o_c")
             nc.vector.scalar_tensor_tensor(
-                out=o_c[:],
-                in0=r_all[:, half * n : (half + 1) * n],
+                out=o_c[:, 0:n],
+                in0=r_bank[s][:, P * a0 : P * a1],
                 scalar=wsn[:, 0:1],
-                in1=t1_tiles[k][:].rearrange("p t i -> p (t i)")[:, half * n : (half + 1) * n],
+                in1=t1_tiles[s][:].rearrange("p t i -> p (t i)")[:, P * a0 : P * a1],
                 op0=ALU.mult,
                 op1=ALU.add,
             )
-            c0 = k * SC * I + half * n
-            nc.sync.dma_start(out=out_view[:, c0 : c0 + n], in_=o_c[:])
+            c0 = s * SC * I + a0 * P
+            nc.sync.dma_start(out=out_view[:, c0 : c0 + n], in_=o_c[:, 0:n])
 
         transposes(0)
-        for j in range(NJ):
+        for j in range(K):
             abs_instr(0, j, 0, GT)
         copy_out(0, 0)
         copy_out(0, 1)
-        for j in range(NJ):
+        for j in range(K):
             abs_instr(0, j, GT, CH)
         quantise(0)
         nc.vector.tensor_scalar(out=hwb[:], in0=wb_raw[:], scalar1=0.5, scalar2=None, op0=ALU.mult)
@@ -354,41 +363,49 @@ def tile_bsplinekanlayer_t_kernel(tc, x, spline_parameters, w_b, w_s, grad_out, 
         nc.vector.tensor_scalar(out=pqwb[:], in0=wb_raw[:], scalar1=0.25, scalar2=None, op0=ALU.mult)
         nc.vector.tensor_scalar(out=wsn[:], in0=ws_raw[:], scalar1=-INV_H, scalar2=None, op0=ALU.mult)
 
-        tanh_at = {}
+        unary_at = {}
         pool_at = {}
-        for k in range(4):
-            tanh_at[k] = 3 * k + 1
-            for step in range(5):
-                pool_at[(k, step)] = 3 * k + 1 + step // 2
+        for k in range(NS):
+            for step in range(4):
+                unary_at[(k, step)] = 3 * k + 1 + step // 2
+            for step in range(2):
+                pool_at[(k, step)] = 3 * k + 2 + step
 
         for gi in range(NG + 3):
             live = gi < NG
             nxt = gi + 1
+            s, a = gi // GS, gi % GS
             if gi + G_BUFS < NG:
                 load_g(gi + G_BUFS)
             c_next = gi // 2 + 1
             fill = []
             if c_next < NT // CH:
-                fill = list(range(0, 9)) if gi % 2 == 0 else list(range(9, NJ))
+                fill = list(range(0, 8)) if gi % 2 == 0 else list(range(8, K))
             if nxt < NG:
                 transposes(nxt)
             if 0 <= gi - 2 < NG:
                 reduce_group(gi - 2)
-            if 0 <= gi - 3 < NG:
-                turn_back(gi - 3)
-            if 1 <= gi <= NG:
-                last_back(gi - 1)
+            if live and a == 1:
+                x_turn(s)
+            if s >= 1 and a == 2 and s - 1 < NS - 1:
+                turn_back(s - 1, 0, GS)
+            if gi == NG + 1:
+                turn_back(NS - 1, 0, GS - 1)
+            if gi == NG + 2:
+                turn_back(NS - 1, GS - 1, GS)
             if live:
                 row_sums(gi)
-            if 1 <= gi <= NG:
-                last_product(gi - 1)
-            if 0 <= gi - 2 < NG:
-                acc_copy(gi - 2)
-            for k in range(4):
-                if gi == 4 * k + 4:
-                    finish(k, 0)
-                if gi == 4 * k + 6:
-                    finish(k, 1)
+            if s >= 1 and a == 1 and s - 1 < NS - 1:
+                sum_t(s - 1, 0, GS)
+            if s >= 1 and a == 2 and s - 1 < NS - 1:
+                finish(s - 1, 0, GS)
+            if gi == NG:
+                sum_t(NS - 1, 0, GS - 1)
+            if gi == NG + 1:
+                finish(NS - 1, 0, GS - 1)
+                sum_t(NS - 1, GS - 1, GS)
+            if gi == NG + 2:
+                finish(NS - 1, GS - 1, GS)
             for j in fill[0:3]:
                 abs_instr(c_next, j)
             if nxt < NG:
@@ -399,28 +416,40 @@ def tile_bsplinekanlayer_t_kernel(tc, x, spline_parameters, w_b, w_s, grad_out, 
                 copy_out(nxt, 1)
             if not live:
                 continue
+            if a == 1:
+                abs16(s)
             g1s = None
-            if gi % 4 == 3:
-                g1s = sums_to_rows_a(gi // 4)
+            if a == GS - 1:
+                g1s = sums_to_rows_a(s)
             for j in fill[5:]:
                 abs_instr(c_next, j)
-            for k in range(4):
-                if tanh_at[k] == gi:
-                    dsilu_tanh(k)
-            for t4 in range(GT):
-                mx_tile(gi, t4)
-                if t4 == 1:
-                    last_pass(gi)
-                    last_out(gi)
+            for k in range(NS):
+                for step in range(4):
+                    if unary_at[(k, step)] == gi:
+                        dsilu_scalar(k, step)
+            if a == GS - 1:
+                last_pass(s)
+            for c in range(GT):
+                mx_tile(gi, c)
+                if c == 1:
+                    if gi == NG - 1:
+                        halve(nc.vector, gi, 0, 2)
+                    if a == GS - 1:
+                        sums_to_rows_b(s, g1s)
+                if c == 2:
                     if nxt < NG:
                         quantise(nxt)
-                    halve(gi, 0, 2)
-                    if gi % 4 == 3:
-                        sums_to_rows_b(gi // 4, g1s)
-            halve(gi, 2, 4)
-            for k in range(4):
-                for step in range(5):
+                    if gi == 0:
+                        quantise_z()
+            if gi == NG - 1:
+                halve(nc.vector, gi, 2, 4)
+            else:
+                halve(nc.gpsimd, gi, 0, 4)
+            if a == GS - 1:
+                last_product(s)
+            for k in range(NS):
+                for step in range(2):
                     if pool_at[(k, step)] == gi:
                         dsilu_pool(k, step)
-                if gi == 4 * k + 3:
-                    silu_term(k)
+            if a == GS - 1:
+                silu_term(s)

@@ -40,7 +40,7 @@ def tile_bsplinekanlayer_t_kernel(tc, x, spline_parameters, w_b, w_s, grad_out, 
         ppool = ctx.enter_context(tc.tile_pool(name="ppool", bufs=4))
         small = ctx.enter_context(tc.tile_pool(name="small", bufs=2))
         ps_tp = ctx.enter_context(tc.psum_pool(name="ps_tp", bufs=2))
-        ps_a = ctx.enter_context(tc.psum_pool(name="ps_a", bufs=3))
+        ps_a = ctx.enter_context(tc.psum_pool(name="ps_a", bufs=4))
         ps_m = ctx.enter_context(tc.psum_pool(name="ps_m", bufs=1))
         ctx.enter_context(tc.manual_schedule())
 
@@ -61,7 +61,6 @@ def tile_bsplinekanlayer_t_kernel(tc, x, spline_parameters, w_b, w_s, grad_out, 
         p16 = {}
         sum_sb = {}
         r_bank = {}
-        gsb_tiles = {}
         t1_tiles = {}
 
         def load_g(gi):
@@ -93,17 +92,8 @@ def tile_bsplinekanlayer_t_kernel(tc, x, spline_parameters, w_b, w_s, grad_out, 
         make_identity(nc, ident[:])
         ident_bf = const.tile([P, P], BF16)
         make_identity(nc, ident_bf[:])
-        ones = const.tile([P, 2], BF16)
-        nc.vector.memset(ones[:], 1.0)
-        sel = const.tile([P, 4, P], F32)
-        nc.vector.memset(sel[:], 0.0)
-        a32 = const.tile([P, 32], F32)
-        nc.vector.tensor_reduce(
-            out=a32[:], in_=ident[:].rearrange("p (b t) -> p b t", t=4), axis=AX.X, op=ALU.add
-        )
-        for h in range(4):
-            nc.vector.tensor_copy(out=sel[:, h, 32 * h : 32 * h + 32], in_=a32[:])
-        g1 = ps_m.tile([P, 5 * SC], F32, name="g1")
+        gsum = const.tile([P, NT], F32)
+        junk = const.tile([P, O], BF16)
 
         pos = const.tile([P, 4 * O], BF16, align_bytes=64)
         neg = const.tile([P, 4 * O], BF16, align_bytes=64)
@@ -187,17 +177,12 @@ def tile_bsplinekanlayer_t_kernel(tc, x, spline_parameters, w_b, w_s, grad_out, 
                 )
 
         def row_sums(gi):
-            for t4 in range(GT):
-                tl = (gi % GS) * GT + t4
-                for h in range(4):
-                    col = h * SC + tl
-                    nc.tensor.matmul(
-                        out=g1[:, col : col + 1],
-                        lhsT=grp[gi][:, O * t4 + P * h : O * t4 + P * h + P],
-                        rhs=ones[:, 0:1],
-                        start=True,
-                        stop=True,
-                    )
+            for c in range(GT):
+                col = gi * GT + c
+                nc.vector.tensor_scalar(
+                    out=junk[:], in0=g_nat[gi][:, O * c : O * c + O], scalar1=1.0, scalar2=None,
+                    op0=ALU.mult, op1=ALU.add, accum_out=gsum[:, col : col + 1],
+                )
 
         def mx_tile(gi, c):
             s, a = gi // GS, gi % GS
@@ -313,26 +298,12 @@ def tile_bsplinekanlayer_t_kernel(tc, x, spline_parameters, w_b, w_s, grad_out, 
             else:
                 nc.gpsimd.tensor_tensor(out=dsw[:, cs], in0=q[:, cs], in1=th[:, cs], op=ALU.add)
 
-        def sums_to_rows_a(k):
-            g1s = small.tile([P, 4 * SC], F32, name="g1s")
-            nc.scalar.copy(out=g1s[:], in_=g1[:, 0 : 4 * SC])
-            return g1s
-
-        def sums_to_rows_b(k, g1s):
-            for h in range(4):
-                nc.tensor.matmul(
-                    out=g1[:, 4 * SC : 5 * SC], lhsT=sel[:, h, :],
-                    rhs=g1s[:, h * SC : (h + 1) * SC], start=(h == 0), stop=(h == 3),
-                )
-            gsb_tiles[k] = small.tile([P, SC], F32, name="gsb")
-            nc.scalar.copy(out=gsb_tiles[k][:], in_=g1[:, 4 * SC : 5 * SC])
-
         def silu_term(k):
             t1_tiles[k] = small.tile([P, SC, I], F32, name="t1")
             nc.gpsimd.tensor_tensor(
                 out=t1_tiles[k][:],
                 in0=dsw[:, k * SC * I : (k + 1) * SC * I].rearrange("p (t i) -> p t i", i=I),
-                in1=gsb_tiles[k][:].unsqueeze(2).to_broadcast([P, SC, I]),
+                in1=gsum[:, k * SC : (k + 1) * SC].unsqueeze(2).to_broadcast([P, SC, I]),
                 op=ALU.mult,
             )
 
@@ -358,6 +329,7 @@ def tile_bsplinekanlayer_t_kernel(tc, x, spline_parameters, w_b, w_s, grad_out, 
         for j in range(K):
             abs_instr(0, j, GT, CH)
         quantise(0)
+        row_sums(0)
         nc.vector.tensor_scalar(out=hwb[:], in0=wb_raw[:], scalar1=0.5, scalar2=None, op0=ALU.mult)
         nc.vector.tensor_scalar(out=nqwb[:], in0=wb_raw[:], scalar1=-0.25, scalar2=None, op0=ALU.mult)
         nc.vector.tensor_scalar(out=pqwb[:], in0=wb_raw[:], scalar1=0.25, scalar2=None, op0=ALU.mult)
@@ -393,8 +365,6 @@ def tile_bsplinekanlayer_t_kernel(tc, x, spline_parameters, w_b, w_s, grad_out, 
                 turn_back(NS - 1, 0, GS - 1)
             if gi == NG + 2:
                 turn_back(NS - 1, GS - 1, GS)
-            if live:
-                row_sums(gi)
             if s >= 1 and a == 1 and s - 1 < NS - 1:
                 sum_t(s - 1, 0, GS)
             if s >= 1 and a == 2 and s - 1 < NS - 1:
@@ -418,9 +388,6 @@ def tile_bsplinekanlayer_t_kernel(tc, x, spline_parameters, w_b, w_s, grad_out, 
                 continue
             if a == 1:
                 abs16(s)
-            g1s = None
-            if a == GS - 1:
-                g1s = sums_to_rows_a(s)
             for j in fill[5:]:
                 abs_instr(c_next, j)
             for k in range(NS):
@@ -434,8 +401,6 @@ def tile_bsplinekanlayer_t_kernel(tc, x, spline_parameters, w_b, w_s, grad_out, 
                 if c == 1:
                     if gi == NG - 1:
                         halve(nc.vector, gi, 0, 2)
-                    if a == GS - 1:
-                        sums_to_rows_b(s, g1s)
                 if c == 2:
                     if nxt < NG:
                         quantise(nxt)
@@ -447,6 +412,8 @@ def tile_bsplinekanlayer_t_kernel(tc, x, spline_parameters, w_b, w_s, grad_out, 
                 halve(nc.gpsimd, gi, 0, 4)
             if a == GS - 1:
                 last_product(s)
+            if nxt < NG:
+                row_sums(nxt)
             for k in range(NS):
                 for step in range(2):
                     if pool_at[(k, step)] == gi:

@@ -77,9 +77,14 @@ def tile_bsplinekanlayer_t_kernel(tc, x, spline_parameters, w_b, w_s, grad_out, 
                 out=praw[:, 2 * u : 2 * u + 2, :],
                 in_=p2d[256 * u : 256 * u + 256, :].rearrange("(q e) c -> q e c", e=2),
             )
-        load_g(0)
+        g_nat[0] = gpool.tile([P, GT * O], BF16, name="g_nat")
+        for half in range(2):
+            nc.sync.dma_start(
+                out=g_nat[0][:, 2 * O * half : 2 * O * (half + 1)], in_=g_view[:, 2 * O * half : 2 * O * (half + 1)]
+            )
+        load_g(1)
         nc.sync.dma_start(out=x_sb[:, CH * I : NT * I], in_=x_view[:, CH * I : NT * I])
-        for gi in range(1, G_BUFS):
+        for gi in range(2, G_BUFS):
             load_g(gi)
         wb_raw = const.tile([P, 1], BF16)
         ws_raw = const.tile([P, 1], BF16)
@@ -95,6 +100,11 @@ def tile_bsplinekanlayer_t_kernel(tc, x, spline_parameters, w_b, w_s, grad_out, 
         gsum = const.tile([P, NT], F32)
         junk = const.tile([P, O], BF16)
 
+        def rows_act(gi):
+            if gi < 2:
+                return 0
+            return 2 if gi < NG - 2 else GT
+
         pos = const.tile([P, 4 * O], BF16, align_bytes=64)
         neg = const.tile([P, 4 * O], BF16, align_bytes=64)
         nc.gpsimd.memset(neg[:, 0 : 4 * I], 0.0)
@@ -102,33 +112,29 @@ def tile_bsplinekanlayer_t_kernel(tc, x, spline_parameters, w_b, w_s, grad_out, 
         nc.vector.tensor_copy(
             out=pos[:].rearrange("p (j i t) -> p j i t", j=K, i=I, t=4), in_=p_perm
         )
-        nc.gpsimd.tensor_scalar(
-            out=neg[:, 4 * I : 4 * O].rearrange("p (j i t) -> p j i t", j=K - 1, i=I, t=4),
-            in0=p_perm[:, 0 : K - 1],
-            scalar1=-1.0,
-            scalar2=0.0,
-            op0=ALU.mult,
-            op1=ALU.add,
+        nc.vector.tensor_scalar(
+            out=neg[:, 4 * I : 4 * O], in0=pos[:, 0 : 4 * (O - I)], scalar1=-1.0, scalar2=None, op0=ALU.mult
         )
         c1 = const.tile([P, O], U32, align_bytes=64)
         s1 = const.tile([P, O], U8, align_bytes=64)
         cn = const.tile([P, O], U32, align_bytes=64)
         sn = const.tile([P, O], U8, align_bytes=64)
         nc.vector.quantize_mx(out=c1[:].bitcast(E4X4), scales=s1[:], in_=pos[:])
-        nc.vector.quantize_mx(out=cn[:].bitcast(E4X4), scales=sn[:], in_=neg[:])
         zsrc = const.tile([P, GT, GT, 4 * I], BF16, align_bytes=64)
         zc = const.tile([P, GT * P], U32, align_bytes=64)
         zs = const.tile([P, GT * P], U8, align_bytes=64)
         nc.gpsimd.memset(zsrc[:], 0.0)
-        for c in range(GT):
-            nc.gpsimd.tensor_scalar(
-                out=zsrc[:, c, c, :].rearrange("p (i t) -> p i t", t=4),
-                in0=p_perm[:, K - 1],
-                scalar1=-1.0,
-                scalar2=0.0,
-                op0=ALU.mult,
-                op1=ALU.add,
-            )
+
+        def fill_z():
+            for c in range(GT):
+                nc.gpsimd.tensor_scalar(
+                    out=zsrc[:, c, c, :],
+                    in0=pos[:, 4 * (O - I) : 4 * O],
+                    scalar1=-1.0,
+                    scalar2=0.0,
+                    op0=ALU.mult,
+                    op1=ALU.add,
+                )
 
         def quantise_z():
             nc.vector.quantize_mx(
@@ -165,23 +171,32 @@ def tile_bsplinekanlayer_t_kernel(tc, x, spline_parameters, w_b, w_s, grad_out, 
                 in_=tp_tiles[(gi, pair)][:].rearrange("p t u b -> p t b u"),
             )
 
-        def quantise(gi):
+        def quantise(gi, c0=0, c1_=GT):
             s, a = gi // GS, gi % GS
-            if a == 0:
+            if a == 0 and c0 == 0:
                 gcode[s] = cpool.tile([P, GT, GS, P], U32, align_bytes=64, name="gc")
                 gscale[s] = cpool.tile([P, GT, GS, P], U8, align_bytes=64, name="gs")
-            for c in range(GT):
+            for c in range(c0, c1_):
                 nc.vector.quantize_mx(
                     out=gcode[s][:, c, a, :].bitcast(E5X4), scales=gscale[s][:, c, a, :],
                     in_=grp[gi][:, O * c : O * c + O],
                 )
 
-        def row_sums(gi):
-            for c in range(GT):
+        def row_sums_scalar(gi):
+            for c in range(rows_act(gi)):
                 col = gi * GT + c
-                nc.vector.tensor_scalar(
-                    out=junk[:], in0=g_nat[gi][:, O * c : O * c + O], scalar1=1.0, scalar2=None,
-                    op0=ALU.mult, op1=ALU.add, accum_out=gsum[:, col : col + 1],
+                nc.scalar.activation(
+                    out=junk[:], in_=g_nat[gi][:, O * c : O * c + O], func=ACT.Copy,
+                    accum_out=gsum[:, col : col + 1],
+                )
+
+        def row_sums_vector(gi):
+            c0 = rows_act(gi)
+            if c0 < GT:
+                nc.vector.tensor_reduce(
+                    out=gsum[:, gi * GT + c0 : (gi + 1) * GT],
+                    in_=g_nat[gi][:, O * c0 : O * GT].rearrange("p (c o) -> p c o", o=O),
+                    axis=AX.X, op=ALU.add,
                 )
 
         def mx_tile(gi, c):
@@ -208,22 +223,15 @@ def tile_bsplinekanlayer_t_kernel(tc, x, spline_parameters, w_b, w_s, grad_out, 
                 op0=ALU.min, op1=ALU.mult,
             )
 
-        def halve(eng, gi, c0, c1_):
-            p_v = p_tiles[gi][:].rearrange("p j t i -> p j (t i)")
-            eng.tensor_tensor(
-                out=p_v[:, 0:8, I * c0 : I * c1_], in0=p_v[:, 0:8, I * c0 : I * c1_],
-                in1=p_v[:, 8:16, I * c0 : I * c1_], op=ALU.add,
-            )
-
         def reduce_group(gi):
             s, a = gi // GS, gi % GS
             if a == 0:
                 acc_t[s] = ps_m.tile([P, GS * P], F32, name="acc_t")
             p_v = p_tiles[gi][:].rearrange("p j t i -> p j (t i)")
-            for j in range(8):
+            for j in range(K):
                 nc.tensor.matmul(
                     out=acc_t[s][:, P * a : P * a + P], lhsT=p_v[:, j, :], rhs=ident[:], is_transpose=True,
-                    start=(j == 0), stop=(j == 7),
+                    start=(j == 0), stop=(j == K - 1),
                 )
 
         def x_turn(s):
@@ -276,25 +284,26 @@ def tile_bsplinekanlayer_t_kernel(tc, x, spline_parameters, w_b, w_s, grad_out, 
         pqwb = const.tile([P, 1], F32)
         wsn = const.tile([P, 1], F32)
 
-        def dsilu_scalar(k, step):
+        def dsilu_tanh(k):
             cs = slice(k * SC * I, (k + 1) * SC * I)
-            if step == 0:
-                nc.scalar.activation(out=th[:, cs], in_=x_sb[:, cs], func=ACT.Tanh, scale=0.5)
-            elif step == 1:
-                nc.scalar.activation(out=q[:, cs], in_=th[:, cs], func=ACT.Square)
-            elif step == 2:
-                nc.scalar.activation(
-                    out=q[:, cs], in_=q[:, cs], func=ACT.Identity, scale=nqwb[:, 0:1], bias=pqwb[:, 0:1]
-                )
-            else:
-                nc.scalar.activation(
-                    out=th[:, cs], in_=th[:, cs], func=ACT.Identity, scale=hwb[:, 0:1], bias=hwb[:, 0:1]
-                )
+            nc.scalar.activation(out=th[:, cs], in_=x_sb[:, cs], func=ACT.Tanh, scale=0.5)
 
         def dsilu_pool(k, step):
             cs = slice(k * SC * I, (k + 1) * SC * I)
             if step == 0:
+                nc.gpsimd.tensor_tensor(out=q[:, cs], in0=th[:, cs], in1=th[:, cs], op=ALU.mult)
+            elif step == 1:
+                nc.gpsimd.tensor_scalar(
+                    out=q[:, cs], in0=q[:, cs], scalar1=nqwb[:, 0:1], scalar2=pqwb[:, 0:1],
+                    op0=ALU.mult, op1=ALU.add,
+                )
+            elif step == 2:
                 nc.gpsimd.tensor_tensor(out=q[:, cs], in0=q[:, cs], in1=x_sb[:, cs], op=ALU.mult)
+            elif step == 3:
+                nc.gpsimd.tensor_scalar(
+                    out=th[:, cs], in0=th[:, cs], scalar1=hwb[:, 0:1], scalar2=hwb[:, 0:1],
+                    op0=ALU.mult, op1=ALU.add,
+                )
             else:
                 nc.gpsimd.tensor_tensor(out=dsw[:, cs], in0=q[:, cs], in1=th[:, cs], op=ALU.add)
 
@@ -326,24 +335,22 @@ def tile_bsplinekanlayer_t_kernel(tc, x, spline_parameters, w_b, w_s, grad_out, 
             abs_instr(0, j, 0, GT)
         copy_out(0, 0)
         copy_out(0, 1)
-        for j in range(K):
-            abs_instr(0, j, GT, CH)
-        quantise(0)
-        row_sums(0)
-        nc.vector.tensor_scalar(out=hwb[:], in0=wb_raw[:], scalar1=0.5, scalar2=None, op0=ALU.mult)
-        nc.vector.tensor_scalar(out=nqwb[:], in0=wb_raw[:], scalar1=-0.25, scalar2=None, op0=ALU.mult)
-        nc.vector.tensor_scalar(out=pqwb[:], in0=wb_raw[:], scalar1=0.25, scalar2=None, op0=ALU.mult)
-        nc.vector.tensor_scalar(out=wsn[:], in0=ws_raw[:], scalar1=-INV_H, scalar2=None, op0=ALU.mult)
+        quantise(0, 0, 1)
+        nc.vector.quantize_mx(out=cn[:].bitcast(E4X4), scales=sn[:], in_=neg[:])
+        quantise(0, 1, GT)
+        row_sums_scalar(0)
+        row_sums_vector(0)
+        for dst, src, factor in ((hwb, wb_raw, 0.5), (nqwb, wb_raw, -0.25), (pqwb, wb_raw, 0.25), (wsn, ws_raw, -INV_H)):
+            nc.gpsimd.tensor_scalar(out=dst[:], in0=src[:], scalar1=factor, scalar2=0.0, op0=ALU.mult, op1=ALU.add)
 
-        unary_at = {}
+        tanh_at = {}
         pool_at = {}
         for k in range(NS):
-            for step in range(4):
-                unary_at[(k, step)] = 3 * k + 1 + step // 2
-            for step in range(2):
-                pool_at[(k, step)] = 3 * k + 2 + step
+            tanh_at[k] = 3 * k + 1
+            for step in range(5):
+                pool_at[(k, step)] = 3 * k + 1 + step // 2
 
-        for gi in range(NG + 3):
+        for gi in range(NG + 1):
             live = gi < NG
             nxt = gi + 1
             s, a = gi // GS, gi % GS
@@ -357,33 +364,43 @@ def tile_bsplinekanlayer_t_kernel(tc, x, spline_parameters, w_b, w_s, grad_out, 
                 transposes(nxt)
             if 0 <= gi - 2 < NG:
                 reduce_group(gi - 2)
+            if gi == NG:
+                reduce_group(NG - 1)
+                sum_t(NS - 1, 0, GS - 1)
+                turn_back(NS - 1, 0, GS - 1)
             if live and a == 1:
                 x_turn(s)
             if s >= 1 and a == 2 and s - 1 < NS - 1:
                 turn_back(s - 1, 0, GS)
-            if gi == NG + 1:
-                turn_back(NS - 1, 0, GS - 1)
-            if gi == NG + 2:
-                turn_back(NS - 1, GS - 1, GS)
             if s >= 1 and a == 1 and s - 1 < NS - 1:
                 sum_t(s - 1, 0, GS)
             if s >= 1 and a == 2 and s - 1 < NS - 1:
                 finish(s - 1, 0, GS)
             if gi == NG:
-                sum_t(NS - 1, 0, GS - 1)
-            if gi == NG + 1:
-                finish(NS - 1, 0, GS - 1)
                 sum_t(NS - 1, GS - 1, GS)
-            if gi == NG + 2:
+                turn_back(NS - 1, GS - 1, GS)
+                finish(NS - 1, 0, GS - 1)
                 finish(NS - 1, GS - 1, GS)
-            for j in fill[0:3]:
-                abs_instr(c_next, j)
-            if nxt < NG:
+            if gi == 0:
+                for j in range(0, 6):
+                    abs_instr(0, j, GT, CH)
                 copy_out(nxt, 0)
-            for j in fill[3:5]:
-                abs_instr(c_next, j)
-            if nxt < NG:
+                for j in range(6, 10):
+                    abs_instr(0, j, GT, CH)
                 copy_out(nxt, 1)
+                for j in range(10, K):
+                    abs_instr(0, j, GT, CH)
+                for j in fill[0:5]:
+                    abs_instr(c_next, j)
+            else:
+                for j in fill[0:3]:
+                    abs_instr(c_next, j)
+                if nxt < NG:
+                    copy_out(nxt, 0)
+                for j in fill[3:5]:
+                    abs_instr(c_next, j)
+                if nxt < NG:
+                    copy_out(nxt, 1)
             if not live:
                 continue
             if a == 1:
@@ -391,31 +408,27 @@ def tile_bsplinekanlayer_t_kernel(tc, x, spline_parameters, w_b, w_s, grad_out, 
             for j in fill[5:]:
                 abs_instr(c_next, j)
             for k in range(NS):
-                for step in range(4):
-                    if unary_at[(k, step)] == gi:
-                        dsilu_scalar(k, step)
+                if tanh_at[k] == gi:
+                    dsilu_tanh(k)
+            if nxt < NG:
+                row_sums_scalar(nxt)
             if a == GS - 1:
                 last_pass(s)
             for c in range(GT):
                 mx_tile(gi, c)
-                if c == 1:
-                    if gi == NG - 1:
-                        halve(nc.vector, gi, 0, 2)
                 if c == 2:
                     if nxt < NG:
                         quantise(nxt)
-                    if gi == 0:
+                    if gi == 1:
                         quantise_z()
-            if gi == NG - 1:
-                halve(nc.vector, gi, 2, 4)
-            else:
-                halve(nc.gpsimd, gi, 0, 4)
             if a == GS - 1:
                 last_product(s)
+            if gi == 0:
+                fill_z()
             if nxt < NG:
-                row_sums(nxt)
+                row_sums_vector(nxt)
             for k in range(NS):
-                for step in range(2):
+                for step in range(5):
                     if pool_at[(k, step)] == gi:
                         dsilu_pool(k, step)
             if a == GS - 1:

@@ -67,9 +67,9 @@ def tile_bsplinekanlayer_t_kernel(tc, x, spline_parameters, w_b, w_s, grad_out, 
             g_nat[gi] = gpool.tile([P, GT * O], BF16, name="g_nat")
             nc.sync.dma_start(out=g_nat[gi][:], in_=g_view[:, gi * GT * O : (gi + 1) * GT * O])
 
-        x_sb = const.tile([P, NT * I], BF16)
+        x2 = const.tile([P, 2, NT * I], BF16)
         x_view = x.rearrange("(p t) i -> p (t i)", t=NT)
-        nc.sync.dma_start(out=x_sb[:, 0 : CH * I], in_=x_view[:, 0 : CH * I])
+        nc.sync.dma_start(out=x2[:, 1, 0 : CH * I], in_=x_view[:, 0 : CH * I])
         praw = const.tile([P, 4, O], BF16)
         p2d = spline_parameters.rearrange("o i k -> o (i k)")
         for u in range(2):
@@ -83,7 +83,7 @@ def tile_bsplinekanlayer_t_kernel(tc, x, spline_parameters, w_b, w_s, grad_out, 
                 out=g_nat[0][:, 2 * O * half : 2 * O * (half + 1)], in_=g_view[:, 2 * O * half : 2 * O * (half + 1)]
             )
         load_g(1)
-        nc.sync.dma_start(out=x_sb[:, CH * I : NT * I], in_=x_view[:, CH * I : NT * I])
+        nc.sync.dma_start(out=x2[:, 1, CH * I : NT * I], in_=x_view[:, CH * I : NT * I])
         for gi in range(2, G_BUFS):
             load_g(gi)
         wb_raw = const.tile([P, 1], BF16)
@@ -91,7 +91,15 @@ def tile_bsplinekanlayer_t_kernel(tc, x, spline_parameters, w_b, w_s, grad_out, 
         nc.scalar.dma_start(out=wb_raw[:], in_=w_b.partition_broadcast(P))
         nc.scalar.dma_start(out=ws_raw[:], in_=w_s.partition_broadcast(P))
 
-        x3 = x_sb[:].rearrange("p (t i) -> p t i", i=I)
+        x4 = x2[:].rearrange("p s (t i) -> p s t i", i=I)
+
+        def negate_x(eng, c0, c1_):
+            eng.tensor_scalar(
+                out=x2[:, 0, c0 * CH * I : c1_ * CH * I], in0=x2[:, 1, c0 * CH * I : c1_ * CH * I],
+                scalar1=-1.0, scalar2=0.0, op0=ALU.mult, op1=ALU.add,
+            )
+
+        negate_x(nc.vector, 0, 1)
 
         ident = const.tile([P, P], F32)
         make_identity(nc, ident[:])
@@ -101,9 +109,19 @@ def tile_bsplinekanlayer_t_kernel(tc, x, spline_parameters, w_b, w_s, grad_out, 
         junk = const.tile([P, O], BF16)
 
         def rows_act(gi):
-            if gi < 2:
-                return 0
-            return 2 if gi < NG - 2 else GT
+            return 2
+
+        def rows_at(it):
+            if it < 2:
+                return []
+            if it < NG - 2:
+                return [it - 2]
+            return [2 * it - NG, 2 * it - NG + 1]
+
+        def rows_at_vector(it):
+            first = max(0, it - 2 + sum(1 for e in (NG - 8, NG - 6, NG - 4) if it > e))
+            last = it - 2 + sum(1 for e in (NG - 8, NG - 6, NG - 4) if it >= e)
+            return [r for r in range(first, last + 1) if 0 <= r < NG]
 
         pos = const.tile([P, 4 * O], BF16, align_bytes=64)
         neg = const.tile([P, 4 * O], BF16, align_bytes=64)
@@ -124,6 +142,8 @@ def tile_bsplinekanlayer_t_kernel(tc, x, spline_parameters, w_b, w_s, grad_out, 
         zc = const.tile([P, GT * P], U32, align_bytes=64)
         zs = const.tile([P, GT * P], U8, align_bytes=64)
         nc.gpsimd.memset(zsrc[:], 0.0)
+        negate_x(nc.gpsimd, 1, 2)
+        negate_x(nc.gpsimd, 2, NT // CH)
 
         def fill_z():
             for c in range(GT):
@@ -141,16 +161,27 @@ def tile_bsplinekanlayer_t_kernel(tc, x, spline_parameters, w_b, w_s, grad_out, 
                 out=zc[:].bitcast(E4X4), scales=zs[:], in_=zsrc[:].rearrange("p a b w -> p (a b w)")
             )
 
-        def abs_instr(c, j, lo=0, hi=CH):
+        def abs_instr(c, m, lo=0, hi=CH):
             if c not in t_tiles:
                 t_tiles[c] = tpool.tile([P, CH, O], F32, name="Tt")
-            nc.scalar.activation(
-                out=t_tiles[c][:, lo:hi, I * j : I * j + I],
-                in_=x3[:, c * CH + lo : c * CH + hi, :],
-                func=ACT.Abs,
-                scale=INV_H,
-                bias=float(8 - j),
-            )
+            rows = slice(c * CH + lo, c * CH + hi)
+            if 1 <= m <= 7:
+                nc.scalar.activation(
+                    out=t_tiles[c][:, lo:hi, :].rearrange("p t (j i) -> p j t i", i=I)[:, 8 - m : 8 + m + 1 : 2 * m],
+                    in_=x4[:, :, rows, :],
+                    func=ACT.Abs,
+                    scale=INV_H,
+                    bias=float(-m),
+                )
+            else:
+                j = 8 - m
+                nc.scalar.activation(
+                    out=t_tiles[c][:, lo:hi, I * j : I * j + I],
+                    in_=x4[:, 1, rows, :],
+                    func=ACT.Abs,
+                    scale=INV_H,
+                    bias=float(m),
+                )
 
         def transposes(gi):
             gw = g_nat[gi][:].bitcast(F32)
@@ -223,22 +254,37 @@ def tile_bsplinekanlayer_t_kernel(tc, x, spline_parameters, w_b, w_s, grad_out, 
                 op0=ALU.min, op1=ALU.mult,
             )
 
+        def slabs_left(gi):
+            if gi == NG - 1:
+                return K
+            return K - 4 if gi < NG - 4 else K // 2
+
+        def fold(gi):
+            n = slabs_left(gi)
+            if n < K:
+                p_v = p_tiles[gi][:].rearrange("p j t i -> p (j t i)")
+                nc.gpsimd.tensor_tensor(
+                    out=p_v[:, (2 * n - K) * P : n * P], in0=p_v[:, (2 * n - K) * P : n * P], in1=p_v[:, n * P : K * P],
+                    op=ALU.add,
+                )
+
         def reduce_group(gi):
             s, a = gi // GS, gi % GS
             if a == 0:
                 acc_t[s] = ps_m.tile([P, GS * P], F32, name="acc_t")
             p_v = p_tiles[gi][:].rearrange("p j t i -> p j (t i)")
-            for j in range(K):
+            n_slabs = slabs_left(gi)
+            for j in range(n_slabs):
                 nc.tensor.matmul(
                     out=acc_t[s][:, P * a : P * a + P], lhsT=p_v[:, j, :], rhs=ident[:], is_transpose=True,
-                    start=(j == 0), stop=(j == K - 1),
+                    start=(j == 0), stop=(j == n_slabs - 1),
                 )
 
         def x_turn(s):
             x_t[s] = ps_m.tile([P, GS, P], BF16, name="multi")
             for a in range(GS):
                 col = (s * GS + a) * P
-                nc.tensor.transpose(x_t[s][:, a, :], x_sb[:, col : col + P], ident_bf[:])
+                nc.tensor.transpose(x_t[s][:, a, :], x2[:, 1, col : col + P], ident_bf[:])
 
         def abs16(s):
             m16[s] = small.tile([P, GS * P], F32, name="m16")
@@ -286,7 +332,7 @@ def tile_bsplinekanlayer_t_kernel(tc, x, spline_parameters, w_b, w_s, grad_out, 
 
         def dsilu_tanh(k):
             cs = slice(k * SC * I, (k + 1) * SC * I)
-            nc.scalar.activation(out=th[:, cs], in_=x_sb[:, cs], func=ACT.Tanh, scale=0.5)
+            nc.scalar.activation(out=th[:, cs], in_=x2[:, 1, cs], func=ACT.Tanh, scale=0.5)
 
         def dsilu_pool(k, step):
             cs = slice(k * SC * I, (k + 1) * SC * I)
@@ -298,7 +344,7 @@ def tile_bsplinekanlayer_t_kernel(tc, x, spline_parameters, w_b, w_s, grad_out, 
                     op0=ALU.mult, op1=ALU.add,
                 )
             elif step == 2:
-                nc.gpsimd.tensor_tensor(out=q[:, cs], in0=q[:, cs], in1=x_sb[:, cs], op=ALU.mult)
+                nc.gpsimd.tensor_tensor(out=q[:, cs], in0=q[:, cs], in1=x2[:, 1, cs], op=ALU.mult)
             elif step == 3:
                 nc.gpsimd.tensor_scalar(
                     out=th[:, cs], in0=th[:, cs], scalar1=hwb[:, 0:1], scalar2=hwb[:, 0:1],
@@ -331,15 +377,13 @@ def tile_bsplinekanlayer_t_kernel(tc, x, spline_parameters, w_b, w_s, grad_out, 
             nc.sync.dma_start(out=out_view[:, c0 : c0 + n], in_=o_c[:, 0:n])
 
         transposes(0)
-        for j in range(K):
-            abs_instr(0, j, 0, GT)
+        for m in range(9):
+            abs_instr(0, m, 0, GT)
         copy_out(0, 0)
         copy_out(0, 1)
         quantise(0, 0, 1)
         nc.vector.quantize_mx(out=cn[:].bitcast(E4X4), scales=sn[:], in_=neg[:])
         quantise(0, 1, GT)
-        row_sums_scalar(0)
-        row_sums_vector(0)
         for dst, src, factor in ((hwb, wb_raw, 0.5), (nqwb, wb_raw, -0.25), (pqwb, wb_raw, 0.25), (wsn, ws_raw, -INV_H)):
             nc.gpsimd.tensor_scalar(out=dst[:], in0=src[:], scalar1=factor, scalar2=0.0, op0=ALU.mult, op1=ALU.add)
 
@@ -348,18 +392,16 @@ def tile_bsplinekanlayer_t_kernel(tc, x, spline_parameters, w_b, w_s, grad_out, 
         for k in range(NS):
             tanh_at[k] = 3 * k + 1
             for step in range(5):
-                pool_at[(k, step)] = 3 * k + 1 + step // 2
+                pool_at[(k, step)] = 3 * k + 1 + step
 
         for gi in range(NG + 1):
             live = gi < NG
             nxt = gi + 1
             s, a = gi // GS, gi % GS
-            if gi + G_BUFS < NG:
-                load_g(gi + G_BUFS)
             c_next = gi // 2 + 1
             fill = []
             if c_next < NT // CH:
-                fill = list(range(0, 8)) if gi % 2 == 0 else list(range(8, K))
+                fill = [1, 2, 3, 4] if gi % 2 == 0 else [5, 6, 7, 0, 8]
             if nxt < NG:
                 transposes(nxt)
             if 0 <= gi - 2 < NG:
@@ -374,7 +416,7 @@ def tile_bsplinekanlayer_t_kernel(tc, x, spline_parameters, w_b, w_s, grad_out, 
                 turn_back(s - 1, 0, GS)
             if s >= 1 and a == 1 and s - 1 < NS - 1:
                 sum_t(s - 1, 0, GS)
-            if s >= 1 and a == 2 and s - 1 < NS - 1:
+            if s >= 1 and a == 3 and s - 1 < NS - 1:
                 finish(s - 1, 0, GS)
             if gi == NG:
                 sum_t(NS - 1, GS - 1, GS)
@@ -382,38 +424,36 @@ def tile_bsplinekanlayer_t_kernel(tc, x, spline_parameters, w_b, w_s, grad_out, 
                 finish(NS - 1, 0, GS - 1)
                 finish(NS - 1, GS - 1, GS)
             if gi == 0:
-                for j in range(0, 6):
-                    abs_instr(0, j, GT, CH)
+                for m in range(0, 3):
+                    abs_instr(0, m, GT, CH)
                 copy_out(nxt, 0)
-                for j in range(6, 10):
-                    abs_instr(0, j, GT, CH)
+                for m in range(3, 5):
+                    abs_instr(0, m, GT, CH)
                 copy_out(nxt, 1)
-                for j in range(10, K):
-                    abs_instr(0, j, GT, CH)
-                for j in fill[0:5]:
-                    abs_instr(c_next, j)
+                for m in range(5, 9):
+                    abs_instr(0, m, GT, CH)
+                for m in fill[0:2]:
+                    abs_instr(c_next, m)
             else:
-                for j in fill[0:3]:
-                    abs_instr(c_next, j)
+                for m in fill[0:1]:
+                    abs_instr(c_next, m)
                 if nxt < NG:
                     copy_out(nxt, 0)
-                for j in fill[3:5]:
-                    abs_instr(c_next, j)
+                for m in fill[1:2]:
+                    abs_instr(c_next, m)
                 if nxt < NG:
                     copy_out(nxt, 1)
             if not live:
                 continue
             if a == 1:
                 abs16(s)
-            for j in fill[5:]:
-                abs_instr(c_next, j)
+            for m in fill[2:]:
+                abs_instr(c_next, m)
             for k in range(NS):
                 if tanh_at[k] == gi:
                     dsilu_tanh(k)
-            if nxt < NG:
-                row_sums_scalar(nxt)
-            if a == GS - 1:
-                last_pass(s)
+            for r in rows_at(gi):
+                row_sums_scalar(r)
             for c in range(GT):
                 mx_tile(gi, c)
                 if c == 2:
@@ -422,14 +462,22 @@ def tile_bsplinekanlayer_t_kernel(tc, x, spline_parameters, w_b, w_s, grad_out, 
                     if gi == 1:
                         quantise_z()
             if a == GS - 1:
-                last_product(s)
+                last_pass(s)
+            fold(gi)
             if gi == 0:
                 fill_z()
-            if nxt < NG:
-                row_sums_vector(nxt)
+            for r in rows_at_vector(gi):
+                row_sums_vector(r)
+            if a == GS - 1:
+                last_product(s)
+            for r in rows_at(gi):
+                if r + G_BUFS < NG:
+                    load_g(r + G_BUFS)
             for k in range(NS):
                 for step in range(5):
                     if pool_at[(k, step)] == gi:
                         dsilu_pool(k, step)
-            if a == GS - 1:
-                silu_term(s)
+            if a == 1 and s >= 1:
+                silu_term(s - 1)
+            if gi == NG - 1:
+                silu_term(NS - 1)

@@ -119,8 +119,8 @@ def tile_bsplinekanlayer_t_kernel(tc, x, spline_parameters, w_b, w_s, grad_out, 
             return [2 * it - NG, 2 * it - NG + 1]
 
         def rows_at_vector(it):
-            first = max(0, it - 2 + sum(1 for e in (NG - 8, NG - 6, NG - 4) if it > e))
-            last = it - 2 + sum(1 for e in (NG - 8, NG - 6, NG - 4) if it >= e)
+            first = max(0, it - 2 + sum(1 for e in (3, 5, 7) if it > e))
+            last = it - 2 + sum(1 for e in (3, 5, 7) if it >= e)
             return [r for r in range(first, last + 1) if 0 <= r < NG]
 
         pos = const.tile([P, 4 * O], BF16, align_bytes=64)

from contextlib import ExitStack

import concourse.mybir as mybir
from concourse.masks import make_identity

F32 = mybir.dt.float32
BF16 = mybir.dt.bfloat16
U32 = mybir.dt.uint32
U8 = mybir.dt.uint8
I32 = mybir.dt.int32
E4X4 = mybir.dt.float8_e4m3fn_x4
E5X4 = mybir.dt.float8_e5m2_x4
ALU = mybir.AluOpType
ACT = mybir.ActivationFunctionType
AX = mybir.AxisListType

P = 128
B, I, O, K = 8192, 32, 512, 16
NT = B // P
GT = 4
GS = 4
CH = 8
SC = GT * GS
NG = NT // GT
NS = NT // SC
INV_H = 57.0 / 7.0
G_BUFS = 6

FLOPS = 2 * B * O * I * K


def tile_bsplinekanlayer_t_kernel(tc, x, spline_parameters, w_b, w_s, grad_out, out):
    nc = tc.nc
    with ExitStack() as ctx:
        const = ctx.enter_context(tc.tile_pool(name="const", bufs=1))
        gpool = ctx.enter_context(tc.tile_pool(name="gpool", bufs=G_BUFS))
        grpool = ctx.enter_context(tc.tile_pool(name="grpool", bufs=3))
        cpool = ctx.enter_context(tc.tile_pool(name="cpool", bufs=2))
        tpool = ctx.enter_context(tc.tile_pool(name="tpool", bufs=3))
        ppool = ctx.enter_context(tc.tile_pool(name="ppool", bufs=4))
        small = ctx.enter_context(tc.tile_pool(name="small", bufs=2))
        ps_tp = ctx.enter_context(tc.psum_pool(name="ps_tp", bufs=2))
        ps_a = ctx.enter_context(tc.psum_pool(name="ps_a", bufs=4))
        ps_m = ctx.enter_context(tc.psum_pool(name="ps_m", bufs=1))
        ctx.enter_context(tc.manual_schedule())

        g_view = grad_out.rearrange("(p t) o -> p (t o)", t=NT)
        out_view = out.rearrange("(p t) i -> p (t i)", t=NT)

        g_nat = {}
        grp = {}
        gcode = {}
        gscale = {}
        t_tiles = {}
        p_tiles = {}
        tp_tiles = {}
        acc_t = {}
        x_t = {}
        m16 = {}
        b16 = {}
        p16 = {}
        sum_sb = {}
        r_bank = {}
        t1_tiles = {}

        def load_g(gi):
            g_nat[gi] = gpool.tile([P, GT * O], BF16, name="g_nat")
            nc.sync.dma_start(out=g_nat[gi][:], in_=g_view[:, gi * GT * O : (gi + 1) * GT * O])

        x2 = const.tile([P, 2, NT * I], BF16)
        x_view = x.rearrange("(p t) i -> p (t i)", t=NT)
        nc.sync.dma_start(out=x2[:, 1, 0 : CH * I], in_=x_view[:, 0 : CH * I])
        praw = const.tile([P, 4, O], BF16)
        p2d = spline_parameters.rearrange("o i k -> o (i k)")
        for u in range(2):
            nc.sync.dma_start(
                out=praw[:, 2 * u : 2 * u + 2, :],
                in_=p2d[256 * u : 256 * u + 256, :].rearrange("(q e) c -> q e c", e=2),
            )
        g_nat[0] = gpool.tile([P, GT * O], BF16, name="g_nat")
        for half in range(2):
            nc.sync.dma_start(
                out=g_nat[0][:, 2 * O * half : 2 * O * (half + 1)], in_=g_view[:, 2 * O * half : 2 * O * (half + 1)]
            )
        load_g(1)
        nc.sync.dma_start(out=x2[:, 1, CH * I : NT * I], in_=x_view[:, CH * I : NT * I])
        for gi in range(2, G_BUFS):
            load_g(gi)
        wb_raw = const.tile([P, 1], BF16)
        ws_raw = const.tile([P, 1], BF16)
        nc.scalar.dma_start(out=wb_raw[:], in_=w_b.partition_broadcast(P))
        nc.scalar.dma_start(out=ws_raw[:], in_=w_s.partition_broadcast(P))

        x4 = x2[:].rearrange("p s (t i) -> p s t i", i=I)

        def negate_x(eng, c0, c1_):
            eng.tensor_scalar(
                out=x2[:, 0, c0 * CH * I : c1_ * CH * I], in0=x2[:, 1, c0 * CH * I : c1_ * CH * I],
                scalar1=-1.0, scalar2=0.0, op0=ALU.mult, op1=ALU.add,
            )

        negate_x(nc.vector, 0, 1)

        ident = const.tile([P, P], F32)
        make_identity(nc, ident[:])
        ident_bf = const.tile([P, P], BF16)
        make_identity(nc, ident_bf[:])
        gsum = const.tile([P, NT], F32)
        junk = const.tile([P, O], BF16)

        def rows_act(gi):
            return 2

        def rows_at(it):
            if it < 2:
                return []
            if it < NG - 2:
                return [it - 2]
            return [2 * it - NG, 2 * it - NG + 1]

        def rows_at_vector(it):
            first = max(0, it - 2 + sum(1 for e in (3, 5, 7) if it > e))
            last = it - 2 + sum(1 for e in (3, 5, 7) if it >= e)
            return [r for r in range(first, last + 1) if 0 <= r < NG]

        pos = const.tile([P, 4 * O], BF16, align_bytes=64)
        neg = const.tile([P, 4 * O], BF16, align_bytes=64)
        nc.gpsimd.memset(neg[:, 0 : 4 * I], 0.0)
        p_perm = praw[:].rearrange("p t (i k) -> p k i t", k=K)
        nc.vector.tensor_copy(
            out=pos[:].rearrange("p (j i t) -> p j i t", j=K, i=I, t=4), in_=p_perm
        )
        nc.vector.tensor_scalar(
            out=neg[:, 4 * I : 4 * O], in0=pos[:, 0 : 4 * (O - I)], scalar1=-1.0, scalar2=None, op0=ALU.mult
        )
        c1 = const.tile([P, O], U32, align_bytes=64)
        s1 = const.tile([P, O], U8, align_bytes=64)
        cn = const.tile([P, O], U32, align_bytes=64)
        sn = const.tile([P, O], U8, align_bytes=64)
        nc.vector.quantize_mx(out=c1[:].bitcast(E4X4), scales=s1[:], in_=pos[:])
        zsrc = const.tile([P, GT, GT, 4 * I], BF16, align_bytes=64)
        zc = const.tile([P, GT * P], U32, align_bytes=64)
        zs = const.tile([P, GT * P], U8, align_bytes=64)
        nc.gpsimd.memset(zsrc[:], 0.0)
        negate_x(nc.gpsimd, 1, 2)
        negate_x(nc.gpsimd, 2, NT // CH)

        def fill_z():
            for c in range(GT):
                nc.gpsimd.tensor_scalar(
                    out=zsrc[:, c, c, :],
                    in0=pos[:, 4 * (O - I) : 4 * O],
                    scalar1=-1.0,
                    scalar2=0.0,
                    op0=ALU.mult,
                    op1=ALU.add,
                )

        def quantise_z():
            nc.vector.quantize_mx(
                out=zc[:].bitcast(E4X4), scales=zs[:], in_=zsrc[:].rearrange("p a b w -> p (a b w)")
            )

        def abs_instr(c, m, lo=0, hi=CH):
            if c not in t_tiles:
                t_tiles[c] = tpool.tile([P, CH, O], F32, name="Tt")
            rows = slice(c * CH + lo, c * CH + hi)
            if 1 <= m <= 7:
                nc.scalar.activation(
                    out=t_tiles[c][:, lo:hi, :].rearrange("p t (j i) -> p j t i", i=I)[:, 8 - m : 8 + m + 1 : 2 * m],
                    in_=x4[:, :, rows, :],
                    func=ACT.Abs,
                    scale=INV_H,
                    bias=float(-m),
                )
            else:
                j = 8 - m
                nc.scalar.activation(
                    out=t_tiles[c][:, lo:hi, I * j : I * j + I],
                    in_=x4[:, 1, rows, :],
                    func=ACT.Abs,
                    scale=INV_H,
                    bias=float(m),
                )

        def transposes(gi):
            gw = g_nat[gi][:].bitcast(F32)
            for pair in range(2):
                tp = ps_tp.tile([P, 2, 2, P], F32, name="tp")
                tp_tiles[(gi, pair)] = tp
                for t2 in range(2):
                    for u in range(2):
                        col = (2 * pair + t2) * 256 + 128 * u
                        nc.tensor.transpose(tp[:, t2, u, :], gw[:, col : col + 128], ident[:])

        def copy_out(gi, pair):
            if pair == 0:
                grp[gi] = grpool.tile([P, GT * O], BF16, align_bytes=64, name="grp")
            grp_w = grp[gi][:].bitcast(F32).rearrange("p (t b u) -> p t b u", t=GT, u=2)
            nc.scalar.copy(
                out=grp_w[:, 2 * pair : 2 * pair + 2],
                in_=tp_tiles[(gi, pair)][:].rearrange("p t u b -> p t b u"),
            )

        def quantise(gi, c0=0, c1_=GT):
            s, a = gi // GS, gi % GS
            if a == 0 and c0 == 0:
                gcode[s] = cpool.tile([P, GT, GS, P], U32, align_bytes=64, name="gc")
                gscale[s] = cpool.tile([P, GT, GS, P], U8, align_bytes=64, name="gs")
            for c in range(c0, c1_):
                nc.vector.quantize_mx(
                    out=gcode[s][:, c, a, :].bitcast(E5X4), scales=gscale[s][:, c, a, :],
                    in_=grp[gi][:, O * c : O * c + O],
                )

        def row_sums_scalar(gi):
            for c in range(rows_act(gi)):
                col = gi * GT + c
                nc.scalar.activation(
                    out=junk[:], in_=g_nat[gi][:, O * c : O * c + O], func=ACT.Copy,
                    accum_out=gsum[:, col : col + 1],
                )

        def row_sums_vector(gi):
            c0 = rows_act(gi)
            if c0 < GT:
                nc.vector.tensor_reduce(
                    out=gsum[:, gi * GT + c0 : (gi + 1) * GT],
                    in_=g_nat[gi][:, O * c0 : O * GT].rearrange("p (c o) -> p c o", o=O),
                    axis=AX.X, op=ALU.add,
                )

        def mx_tile(gi, c):
            s, a = gi // GS, gi % GS
            lhs = gcode[s][:, c, a, :].bitcast(E5X4)
            lhs_s = gscale[s][:, c, a, :]
            bank_a = ps_a.tile([P, O], F32, name="bank_a")
            nc.tensor.matmul_mx(
                out=bank_a[:], lhsT=lhs, lhsT_scale=lhs_s,
                rhs=c1[:].bitcast(E4X4), rhs_scale=s1[:], start=True, stop=False,
            )
            nc.tensor.matmul_mx(
                out=bank_a[:], lhsT=lhs, lhsT_scale=lhs_s,
                rhs=cn[:].bitcast(E4X4), rhs_scale=sn[:], start=False, stop=True,
            )
            if c == 0:
                p_tiles[gi] = ppool.tile([P, K, GT, I], F32, name="p_t")
            tile_no = gi * GT + c
            nc.vector.scalar_tensor_tensor(
                out=p_tiles[gi][:, :, c, :],
                in0=t_tiles[tile_no // CH][:, tile_no % CH, :].rearrange("p (j i) -> p j i", i=I),
                scalar=1.0,
                in1=bank_a[:].rearrange("p (j i) -> p j i", i=I),
                op0=ALU.min, op1=ALU.mult,
            )

        def slabs_left(gi):
            if gi == NG - 1:
                return K
            return K - 4 if gi < NG - 4 else K // 2

        def fold(gi):
            n = slabs_left(gi)
            if n < K:
                p_v = p_tiles[gi][:].rearrange("p j t i -> p (j t i)")
                nc.gpsimd.tensor_tensor(
                    out=p_v[:, (2 * n - K) * P : n * P], in0=p_v[:, (2 * n - K) * P : n * P], in1=p_v[:, n * P : K * P],
                    op=ALU.add,
                )

        def reduce_group(gi):
            s, a = gi // GS, gi % GS
            if a == 0:
                acc_t[s] = ps_m.tile([P, GS * P], F32, name="acc_t")
            p_v = p_tiles[gi][:].rearrange("p j t i -> p j (t i)")
            n_slabs = slabs_left(gi)
            for j in range(n_slabs):
                nc.tensor.matmul(
                    out=acc_t[s][:, P * a : P * a + P], lhsT=p_v[:, j, :], rhs=ident[:], is_transpose=True,
                    start=(j == 0), stop=(j == n_slabs - 1),
                )

        def x_turn(s):
            x_t[s] = ps_m.tile([P, GS, P], BF16, name="multi")
            for a in range(GS):
                col = (s * GS + a) * P
                nc.tensor.transpose(x_t[s][:, a, :], x2[:, 1, col : col + P], ident_bf[:])

        def abs16(s):
            m16[s] = small.tile([P, GS * P], F32, name="m16")
            nc.scalar.activation(
                out=m16[s][:], in_=x_t[s][:].rearrange("p a b -> p (a b)"), func=ACT.Abs,
                scale=INV_H, bias=float(8 - K),
            )

        def last_pass(s):
            b16[s] = ps_m.tile([P, GS * P], F32, name="multi")
            for c in range(GT):
                nc.tensor.matmul_mx(
                    out=b16[s][:],
                    lhsT=zc[:, P * c : P * c + P].bitcast(E4X4), lhsT_scale=zs[:, P * c : P * c + P],
                    rhs=gcode[s][:, c, :, :].rearrange("p a b -> p (a b)").bitcast(E5X4),
                    rhs_scale=gscale[s][:, c, :, :].rearrange("p a b -> p (a b)"),
                    start=(c == 0), stop=(c == GT - 1),
                )

        def last_product(s):
            p16[s] = small.tile([P, GS * P], F32, name="p16")
            nc.vector.scalar_tensor_tensor(
                out=p16[s][:], in0=m16[s][:], scalar=1.0, in1=b16[s][:], op0=ALU.min, op1=ALU.mult,
            )

        def sum_t(s, a0, a1):
            if s not in sum_sb:
                sum_sb[s] = small.tile([P, GS * P], F32, name="sum_sb")
            cs = slice(P * a0, P * a1)
            nc.vector.tensor_tensor(out=sum_sb[s][:, cs], in0=acc_t[s][:, cs], in1=p16[s][:, cs], op=ALU.add)

        def turn_back(s, a0, a1):
            if s not in r_bank:
                r_bank[s] = ps_m.tile([P, GS * P], F32, name="multi")
            for a in range(a0, a1):
                nc.tensor.transpose(r_bank[s][:, P * a : P * a + P], sum_sb[s][:, P * a : P * a + P], ident[:])

        th = const.tile([P, NT * I], F32)
        q = const.tile([P, NT * I], F32)
        dsw = const.tile([P, NT * I], F32)
        hwb = const.tile([P, 1], F32)
        nqwb = const.tile([P, 1], F32)
        pqwb = const.tile([P, 1], F32)
        wsn = const.tile([P, 1], F32)

        def dsilu_tanh(k):
            cs = slice(k * SC * I, (k + 1) * SC * I)
            nc.scalar.activation(out=th[:, cs], in_=x2[:, 1, cs], func=ACT.Tanh, scale=0.5)

        def dsilu_pool(k, step):
            cs = slice(k * SC * I, (k + 1) * SC * I)
            if step == 0:
                nc.gpsimd.tensor_tensor(out=q[:, cs], in0=th[:, cs], in1=th[:, cs], op=ALU.mult)
            elif step == 1:
                nc.gpsimd.tensor_scalar(
                    out=q[:, cs], in0=q[:, cs], scalar1=nqwb[:, 0:1], scalar2=pqwb[:, 0:1],
                    op0=ALU.mult, op1=ALU.add,
                )
            elif step == 2:
                nc.gpsimd.tensor_tensor(out=q[:, cs], in0=q[:, cs], in1=x2[:, 1, cs], op=ALU.mult)
            elif step == 3:
                nc.gpsimd.tensor_scalar(
                    out=th[:, cs], in0=th[:, cs], scalar1=hwb[:, 0:1], scalar2=hwb[:, 0:1],
                    op0=ALU.mult, op1=ALU.add,
                )
            else:
                nc.gpsimd.tensor_tensor(out=dsw[:, cs], in0=q[:, cs], in1=th[:, cs], op=ALU.add)

        def silu_term(k):
            t1_tiles[k] = small.tile([P, SC, I], F32, name="t1")
            nc.gpsimd.tensor_tensor(
                out=t1_tiles[k][:],
                in0=dsw[:, k * SC * I : (k + 1) * SC * I].rearrange("p (t i) -> p t i", i=I),
                in1=gsum[:, k * SC : (k + 1) * SC].unsqueeze(2).to_broadcast([P, SC, I]),
                op=ALU.mult,
            )

        def finish(s, a0, a1):
            n = (a1 - a0) * P
            o_c = small.tile([P, GS * P], F32, name="o_c")
            nc.vector.scalar_tensor_tensor(
                out=o_c[:, 0:n],
                in0=r_bank[s][:, P * a0 : P * a1],
                scalar=wsn[:, 0:1],
                in1=t1_tiles[s][:].rearrange("p t i -> p (t i)")[:, P * a0 : P * a1],
                op0=ALU.mult,
                op1=ALU.add,
            )
            c0 = s * SC * I + a0 * P
            nc.sync.dma_start(out=out_view[:, c0 : c0 + n], in_=o_c[:, 0:n])

        transposes(0)
        for m in range(9):
            abs_instr(0, m, 0, GT)
        copy_out(0, 0)
        copy_out(0, 1)
        quantise(0, 0, 1)
        nc.vector.quantize_mx(out=cn[:].bitcast(E4X4), scales=sn[:], in_=neg[:])
        quantise(0, 1, GT)
        for dst, src, factor in ((hwb, wb_raw, 0.5), (nqwb, wb_raw, -0.25), (pqwb, wb_raw, 0.25), (wsn, ws_raw, -INV_H)):
            nc.gpsimd.tensor_scalar(out=dst[:], in0=src[:], scalar1=factor, scalar2=0.0, op0=ALU.mult, op1=ALU.add)

        tanh_at = {}
        pool_at = {}
        for k in range(NS):
            tanh_at[k] = 3 * k + 1
            for step in range(5):
                pool_at[(k, step)] = 3 * k + 1 + step

        for gi in range(NG + 1):
            live = gi < NG
            nxt = gi + 1
            s, a = gi // GS, gi % GS
            c_next = gi // 2 + 1
            fill = []
            if c_next < NT // CH:
                fill = [1, 2, 3, 4] if gi % 2 == 0 else [5, 6, 7, 0, 8]
            if nxt < NG:
                transposes(nxt)
            if 0 <= gi - 2 < NG:
                reduce_group(gi - 2)
            if gi == NG:
                reduce_group(NG - 1)
                sum_t(NS - 1, 0, GS - 1)
                turn_back(NS - 1, 0, GS - 1)
            if live and a == 1:
                x_turn(s)
            if s >= 1 and a == 2 and s - 1 < NS - 1:
                turn_back(s - 1, 0, GS)
            if s >= 1 and a == 1 and s - 1 < NS - 1:
                sum_t(s - 1, 0, GS)
            if s >= 1 and a == 3 and s - 1 < NS - 1:
                finish(s - 1, 0, GS)
            if gi == NG:
                sum_t(NS - 1, GS - 1, GS)
                turn_back(NS - 1, GS - 1, GS)
                finish(NS - 1, 0, GS - 1)
                finish(NS - 1, GS - 1, GS)
            if gi == 0:
                for m in range(0, 3):
                    abs_instr(0, m, GT, CH)
                copy_out(nxt, 0)
                for m in range(3, 5):
                    abs_instr(0, m, GT, CH)
                copy_out(nxt, 1)
                for m in range(5, 9):
                    abs_instr(0, m, GT, CH)
                for m in fill[0:2]:
                    abs_instr(c_next, m)
            else:
                for m in fill[0:1]:
                    abs_instr(c_next, m)
                if nxt < NG:
                    copy_out(nxt, 0)
                for m in fill[1:2]:
                    abs_instr(c_next, m)
                if nxt < NG:
                    copy_out(nxt, 1)
            if not live:
                continue
            if a == 1:
                abs16(s)
            for m in fill[2:]:
                abs_instr(c_next, m)
            for k in range(NS):
                if tanh_at[k] == gi:
                    dsilu_tanh(k)
            for r in rows_at(gi):
                row_sums_scalar(r)
            for c in range(GT):
                mx_tile(gi, c)
                if c == 2:
                    if nxt < NG:
                        quantise(nxt)
                    if gi == 1:
                        quantise_z()
            if a == GS - 1:
                last_pass(s)
            fold(gi)
            if gi == 0:
                fill_z()
            for r in rows_at_vector(gi):
                row_sums_vector(r)
            if a == GS - 1:
                last_product(s)
            for r in rows_at(gi):
                if r + G_BUFS < NG:
                    load_g(r + G_BUFS)
            for k in range(NS):
                for step in range(5):
                    if pool_at[(k, step)] == gi:
                        dsilu_pool(k, step)
            if a == 1 and s >= 1:
                silu_term(s - 1)
            if gi == NG - 1:
                silu_term(NS - 1)
